import numpy as np
import ml_dtypes


def mxq(x, axis, fmt="e4m3"):
    dtype, down = {"e4m3": (ml_dtypes.float8_e4m3fn, 7), "e5m2": (ml_dtypes.float8_e5m2, 14)}[fmt]
    v = np.moveaxis(np.asarray(x, np.float32).astype(ml_dtypes.bfloat16).astype(np.float64), axis, -1)
    blocks = v.reshape(v.shape[:-1] + (-1, 32))
    amax = np.abs(blocks).max(-1, keepdims=True)
    byte = np.maximum(np.where(amax > 0, np.frexp(amax)[1] - 1 + 127, 0) - down, 1)
    scale = np.exp2(byte - 127.0)
    codes = (blocks / scale).astype(np.float32).astype(dtype).astype(np.float64)
    return np.moveaxis((codes * scale).reshape(v.shape), -1, axis)


WIDE = False


def mx_kscale(k):
    if not WIDE:
        return np.ones(k)
    levels = np.array([10, -10, 5, -5, 0])
    a = np.random.permutation(np.resize(levels, k // 512 * 4)).reshape(k // 512, 4)
    idx = np.arange(k)
    return np.exp2(a[idx // 512, idx % 128 // 32])


BF16 = ml_dtypes.bfloat16


def bf(x):
    return np.asarray(x, np.float32).astype(BF16)


def f64(x):
    return np.asarray(x).astype(np.float64)


E2M1 = np.array([0.0, 0.5, 1.0, 1.5, 2.0, 3.0, 4.0, 6.0, -0.0, -0.5, -1.0, -1.5, -2.0, -3.0, -4.0, -6.0])


def pack_weight(w, fmt):
    k, n = w.shape
    w = f64(bf(w)).reshape(k // 32, 32, n)
    amax = np.abs(w).max(1)
    if fmt == "e4m3":
        byte = np.frexp(amax)[1] - 1 + 127 - 7
    else:
        mant, ex = np.frexp(amax / 6.0)
        byte = np.where(mant > 0.5, ex, ex - 1) + 127
    byte = np.clip(np.where(amax > 0, byte, 1), 1, 254)
    scaled = (w * np.exp2(127.0 - byte)[:, None, :]).reshape(k, n).astype(np.float32)
    by_word = np.ascontiguousarray(scaled.reshape(k // 512, 128, 4, n).transpose(0, 1, 3, 2))
    if fmt == "e4m3":
        words = by_word.astype(ml_dtypes.float8_e4m3fn).view(np.uint8)
    else:
        c = by_word.astype(ml_dtypes.float4_e2m1fn).view(np.uint8) & 0xF
        words = c[..., 0::2] | (c[..., 1::2] << 4)
    return np.ascontiguousarray(words), np.ascontiguousarray(byte.astype(np.uint8).reshape(k // 512, 16, n))


def unpack_weight(words, scales, fmt):
    g, p, n, _ = words.shape
    if fmt == "e4m3":
        vals = np.ascontiguousarray(words).view(ml_dtypes.float8_e4m3fn).astype(np.float64)
    else:
        nib = np.empty((g, p, n, 4), np.uint8)
        nib[..., 0::2] = words & 0xF
        nib[..., 1::2] = words >> 4
        vals = E2M1[nib]
    vals = vals * np.repeat(np.exp2(scales.astype(np.float64) - 127.0), 8, axis=1)[..., None]
    return vals.transpose(0, 1, 3, 2).reshape(g * 512, n)


B, T, HS, WS, G, K, CB, CB2, CB3, CB4 = 4, 64, 4, 4, 2, 1024, 128, 160, 200, 250
EPS = 1e-3
NV = 5
R = B * T * HS * WS


def bn_apply(v, p):
    gamma, beta, mean, var = p[0], p[1], p[2], p[3]
    return (v - mean) * (gamma / np.sqrt(var + EPS)) + beta


def dwconv_t(v, taps, d):
    vp = np.pad(v, ((0, 0), (d, d), (0, 0), (0, 0), (0, 0), (0, 0)))
    return taps[0] * vp[:, 0:T] + taps[1] * vp[:, d:d + T] + taps[2] * vp[:, 2 * d:2 * d + T]


def setup_inputs():
    s = mx_kscale(K)
    gamma = 1.0 + 0.1 * np.random.standard_normal((NV, G, CB))
    beta = 0.2 * np.random.standard_normal((NV, G, CB))
    mean = 0.04 * np.random.standard_normal((NV, G, CB))
    var = np.random.uniform(0.01, 0.04, (NV, G, CB))
    x = bf(np.random.standard_normal((B, T, HS, WS, G * K)) * np.tile(s, G))
    stack = np.random.standard_normal((NV, G, K, CB)) * 0.15 / np.sqrt(K) / s[:, None]
    words, scales = pack_weight(stack.reshape(-1, CB), "e4m3")
    return {"x": x,
            "w_words": words,
            "w_scales": scales,
            "b": bf(np.random.standard_normal((NV, G, CB)) * 0.04),
            "dw": bf(np.random.standard_normal((3, 3, G, CB)) * 0.6),
            "bn": bf(np.stack([gamma, beta, mean, var], axis=1))}


def reference(x, w_words, w_scales, b, dw, bn):
    b, dw, bn = f64(b), f64(dw), f64(bn)
    xg = f64(x).reshape(R, G, K).transpose(1, 0, 2)
    wg = unpack_weight(w_words, w_scales, "e4m3").reshape(NV, G, K, CB).transpose(1, 2, 0, 3).reshape(G, K, NV * CB)
    y = mxq(xg, 2, "e4m3") @ wg
    y = y.reshape(G, B, T, HS, WS, NV, CB).transpose(5, 1, 2, 3, 4, 0, 6) + b[:, None, None, None, None]
    outs = [bn_apply(y[0], bn[0])]
    for i, d in enumerate((1, 2, 3)):
        outs.append(bn_apply(dwconv_t(y[1 + i], dw[i], d), bn[1 + i]))
    t5 = np.maximum(y[4], np.concatenate([y[4][:, 1:], y[4][:, -1:]], axis=1))
    outs.append(bn_apply(t5, bn[4]))
    z = np.stack(outs, axis=5)
    z = np.maximum(z.reshape(B, T, HS, WS, G * NV * CB), 0.0)
    z = z.reshape(B, T, HS, WS, G, NV * CB).swapaxes(-1, -2).reshape(B, T, HS, WS, G * NV * CB)
    return z.reshape(B, T // 2, 2, HS, WS, G * NV * CB).max(axis=2)

@@ -1,0 +1,236 @@
+from contextlib import ExitStack
+
+import concourse.mybir as mybir
+from concourse.masks import make_identity
+
+F32 = mybir.dt.float32
+BF16 = mybir.dt.bfloat16
+I32 = mybir.dt.int32
+U32 = mybir.dt.uint32
+U8 = mybir.dt.uint8
+FP8X4 = mybir.dt.float8_e4m3fn_x4
+ALU = mybir.AluOpType
+ACT = mybir.ActivationFunctionType
+
+P = 128
+BATCH, TIME, PIXELS = 4, 64, 16
+GROUPS, K, CB, BRANCHES = 2, 1024, 128, 5
+EPS = 1e-3
+K_PASS = 4 * P
+PASSES = K // K_PASS
+X_PASSES = GROUPS * PASSES
+COLS = TIME * PIXELS
+BANK = 512
+CHUNK = 2 * P
+CHUNKS = COLS // CHUNK
+OUT_COLS = COLS // 2
+OUT_CH = GROUPS * BRANCHES * CB
+
+FLOPS = 2 * BATCH * COLS * GROUPS * K * BRANCHES * CB
+
+
+def tile_timeception_pa_t_e_kernel(tc, x, w_words, w_scales, b, dw, bn, out):
+    nc = tc.nc
+    x_rows = x.rearrange("n t h w c -> (n t h w) c")
+    out_rows = out.rearrange("n t h w c -> (n t h w) c")
+
+    with ExitStack() as ctx:
+        const = ctx.enter_context(tc.tile_pool(name="const", bufs=1))
+        x_pool = ctx.enter_context(tc.tile_pool(name="x", bufs=6))
+        grouped_pool = ctx.enter_context(tc.tile_pool(name="grouped", bufs=4))
+        codes_pool = ctx.enter_context(tc.tile_pool(name="codes", bufs=2))
+        work = ctx.enter_context(tc.tile_pool(name="work", bufs=4))
+        pooled_pool = ctx.enter_context(tc.tile_pool(name="pooled", bufs=6))
+        out_pool = ctx.enter_context(tc.tile_pool(name="outp", bufs=2))
+        flip_psum = ctx.enter_context(tc.psum_pool(name="flip", bufs=4))
+        acc_psum = ctx.enter_context(tc.psum_pool(name="acc", bufs=4))
+
+        def load_chunk(chunk):
+            x_tile = x_pool.tile([P, 2, GROUPS * K], BF16, tag="x")
+            rows = x_rows[chunk * CHUNK : (chunk + 1) * CHUNK, :]
+            nc.sync.dma_start(out=x_tile[:], in_=rows.rearrange("(a p) c -> p a c", p=P))
+            return x_tile
+
+        first_x = load_chunk(0)
+
+        w_codes = const.tile([P, BRANCHES * X_PASSES, CB], U32, align_bytes=64)
+        w_planes = const.tile([P, BRANCHES * X_PASSES, CB], U8, align_bytes=64)
+        nc.vector.memset(w_planes[:].bitcast(I32), 0)
+        for quad in range(4):
+            nc.sync.dma_start(
+                out=w_planes[32 * quad : 32 * quad + 4].bitcast(I32),
+                in_=w_scales[:, 4 * quad : 4 * quad + 4, :].bitcast(I32).rearrange("e r o -> r e o"),
+            )
+        nc.sync.dma_start(
+            out=w_codes[:].bitcast(I32),
+            in_=w_words.rearrange("e p o t -> e p (o t)").bitcast(I32).rearrange("e p o -> p e o"),
+        )
+
+        ident = const.tile([P, P], F32)
+        make_identity(nc, ident[:])
+        n_b, n_dw, n_bn = BRANCHES * GROUPS, 3 * 3 * GROUPS, BRANCHES * 4 * GROUPS
+        rows_bf = const.tile([P, CB], BF16)
+        nc.vector.memset(rows_bf[:], 0.0)
+        nc.scalar.dma_start(out=rows_bf[0:n_b, :], in_=b.rearrange("v g o -> (v g) o"))
+        nc.scalar.dma_start(out=rows_bf[n_b : n_b + n_dw, :], in_=dw.rearrange("i k g o -> (i k g) o"))
+        nc.scalar.dma_start(
+            out=rows_bf[n_b + n_dw : n_b + n_dw + n_bn, :], in_=bn.rearrange("v j g o -> (v j g) o")
+        )
+        rows_f32 = const.tile([P, CB], F32)
+        nc.vector.tensor_copy(out=rows_f32[:], in_=rows_bf[:])
+        params_ps = flip_psum.tile([P, BANK], F32, tag="flip")
+        nc.tensor.transpose(params_ps[:, 0:P], rows_f32[:], ident[:])
+        params = const.tile([P, P], F32)
+        nc.vector.tensor_copy(out=params[:], in_=params_ps[:, 0:P])
+        bias = params[:, 0:n_b].rearrange("p (v g) -> p v g", g=GROUPS)
+        taps = params[:, n_b : n_b + n_dw].rearrange("p (i k g) -> p i k g", k=3, g=GROUPS)
+        bn_p = params[:, n_b + n_dw : n_b + n_dw + n_bn].rearrange("p (v j g) -> p v j g", j=4, g=GROUPS)
+        gamma, beta, mean, var = bn_p[:, :, 0, :], bn_p[:, :, 1, :], bn_p[:, :, 2, :], bn_p[:, :, 3, :]
+
+        scale = const.tile([P, BRANCHES, GROUPS], F32)
+        nc.vector.tensor_scalar_add(out=scale[:], in0=var, scalar1=EPS)
+        nc.scalar.activation(out=scale[:], in_=scale[:], func=ACT.Sqrt)
+        nc.vector.reciprocal(out=scale[:], in_=scale[:])
+        nc.vector.tensor_mul(out=scale[:], in0=scale[:], in1=gamma)
+        shift = const.tile([P, BRANCHES, GROUPS], F32)
+        nc.vector.tensor_mul(out=shift[:], in0=scale[:], in1=mean)
+        nc.vector.tensor_sub(out=shift[:], in0=beta, in1=shift[:])
+        offset = const.tile([P, BRANCHES, GROUPS], F32)
+        nc.vector.tensor_mul(out=offset[:], in0=scale[:], in1=bias)
+        nc.vector.tensor_add(out=offset[:], in0=offset[:], in1=shift[:])
+        conv_shape = [P, 3, 3, GROUPS]
+        s_taps = const.tile(conv_shape, F32)
+        nc.vector.tensor_mul(out=s_taps[:], in0=taps, in1=scale[:, 1:4, :].unsqueeze(2).to_broadcast(conv_shape))
+        tap_bias = const.tile(conv_shape, F32)
+        nc.vector.tensor_mul(out=tap_bias[:], in0=s_taps[:], in1=bias[:, 1:4, :].unsqueeze(2).to_broadcast(conv_shape))
+        c_inner = const.tile([P, 3, GROUPS], F32)
+        nc.vector.tensor_add(out=c_inner[:], in0=shift[:, 1:4, :], in1=tap_bias[:, :, 1, :])
+        c_first = const.tile([P, 3, GROUPS], F32)
+        nc.vector.tensor_add(out=c_first[:], in0=c_inner[:], in1=tap_bias[:, :, 2, :])
+        c_last = const.tile([P, 3, GROUPS], F32)
+        nc.vector.tensor_add(out=c_last[:], in0=c_inner[:], in1=tap_bias[:, :, 0, :])
+        nc.vector.tensor_add(out=c_inner[:], in0=c_first[:], in1=tap_bias[:, :, 0, :])
+
+        def quantise_chunk(x_tile, x_codes, x_planes, cols):
+            for c in range(X_PASSES):
+                flipped = flip_psum.tile([P, 2, 2, P], F32, tag="flip")
+                for a in range(2):
+                    words = x_tile[:, a, :].bitcast(F32)
+                    for u in range(2):
+                        nc.tensor.transpose(
+                            flipped[:, a, u, :], words[:, 256 * c + u : 256 * (c + 1) : 2], ident[:]
+                        )
+                grouped = grouped_pool.tile([P, 4 * CHUNK], BF16, align_bytes=64)
+                nc.scalar.copy(
+                    out=grouped[:].bitcast(F32).rearrange("p (a r u) -> p a r u", a=2, u=2),
+                    in_=flipped[:].rearrange("p a u r -> p a r u"),
+                )
+                nc.vector.quantize_mx(
+                    out=x_codes[:, c, cols].bitcast(FP8X4), scales=x_planes[:, c, cols], in_=grouped[:]
+                )
+
+        def new_codes():
+            x_codes = codes_pool.tile([P, X_PASSES, COLS], U32, align_bytes=64, tag="codes")
+            x_planes = codes_pool.tile([P, X_PASSES, COLS], U8, align_bytes=64, tag="planes")
+            return x_codes, x_planes
+
+        def multiply(x_codes, x_planes, v, g):
+            early = acc_psum.tile([P, BANK], F32, tag="acc")
+            late = acc_psum.tile([P, BANK], F32, tag="acc")
+            for half, acc in enumerate((early, late)):
+                cols = slice(half * BANK, (half + 1) * BANK)
+                for kp in range(PASSES):
+                    e = (v * GROUPS + g) * PASSES + kp
+                    c = g * PASSES + kp
+                    nc.tensor.matmul_mx(
+                        out=acc[:],
+                        lhsT=w_codes[:, e, :].bitcast(FP8X4),
+                        lhsT_scale=w_planes[:, e, :],
+                        rhs=x_codes[:, c, cols].bitcast(FP8X4),
+                        rhs_scale=x_planes[:, c, cols],
+                        start=(kp == 0),
+                        stop=(kp == PASSES - 1),
+                    )
+            return early, late
+
+        def affine(dst, src, mul, add):
+            nc.scalar.activation(out=dst, in_=src, func=ACT.Identity, scale=mul, bias=add)
+
+        def add_tap(dst, src, tap):
+            nc.vector.scalar_tensor_tensor(out=dst, in0=src, scalar=tap, in1=dst, op0=ALU.mult, op1=ALU.add)
+
+        def branch(early, late, v, g):
+            u = work.tile([P, COLS], F32, tag="u")
+            mul, add = scale[:, v, g : g + 1], offset[:, v, g : g + 1]
+            if v == 0:
+                affine(u[:, 0:BANK], early[:], mul, add)
+                affine(u[:, BANK:COLS], late[:], mul, add)
+            elif v == 4:
+                nc.scalar.copy(out=u[:, 0:BANK], in_=early[:])
+                nc.scalar.copy(out=u[:, BANK:COLS], in_=late[:])
+                s = PIXELS
+                nc.vector.tensor_tensor(out=u[:, 0 : BANK - s], in0=early[:, s:BANK], in1=u[:, 0 : BANK - s], op=ALU.max)
+                nc.vector.tensor_tensor(out=u[:, BANK - s : COLS - s], in0=late[:], in1=u[:, BANK - s : COLS - s], op=ALU.max)
+                affine(u[:], u[:], mul, add)
+            else:
+                i = v - 1
+                s = v * PIXELS
+                before, centre, after = [s_taps[:, i, k, g : g + 1] for k in range(3)]
+                affine(u[:, 0:s], early[:, 0:s], centre, c_first[:, i, g : g + 1])
+                affine(u[:, s:BANK], early[:, s:BANK], centre, c_inner[:, i, g : g + 1])
+                affine(u[:, BANK : COLS - s], late[:, 0 : BANK - s], centre, c_inner[:, i, g : g + 1])
+                affine(u[:, COLS - s : COLS], late[:, BANK - s : BANK], centre, c_last[:, i, g : g + 1])
+                add_tap(u[:, s : s + BANK], early[:], before)
+                add_tap(u[:, s + BANK : COLS], late[:, 0 : BANK - s], before)
+                add_tap(u[:, 0 : BANK - s], early[:, s:BANK], after)
+                add_tap(u[:, BANK - s : COLS - s], late[:], after)
+            pooled = pooled_pool.tile([P, OUT_COLS], F32, tag="pooled")
+            pairs = u[:].rearrange("p (t two q) -> p t two q", two=2, q=PIXELS)
+            nc.vector.tensor_tensor(
+                out=pooled[:].rearrange("p (t q) -> p t q", q=PIXELS), in0=pairs[:, :, 0, :], in1=pairs[:, :, 1, :], op=ALU.max
+            )
+            return pooled
+
+        def emit(out_tile, pooled_by_group, v):
+            for pair in range(OUT_COLS // CHUNK):
+                flipped = flip_psum.tile([P, 2, GROUPS, P], F32, tag="flip")
+                for a in range(2):
+                    first = (2 * pair + a) * P
+                    for g in range(GROUPS):
+                        nc.tensor.transpose(flipped[:, a, g, :], pooled_by_group[g][:, first : first + P], ident[:])
+                channels = out_tile[:, 2 * pair : 2 * pair + 2, v * GROUPS * CB : (v + 1) * GROUPS * CB]
+                nc.scalar.activation(
+                    out=channels.rearrange("p a (o g) -> p a o g", g=GROUPS),
+                    in_=flipped[:].rearrange("p a g o -> p a o g"),
+                    func=ACT.Relu,
+                )
+
+        def store(out_tile, n):
+            rows = out_rows[n * OUT_COLS : (n + 1) * OUT_COLS, :]
+            nc.sync.dma_start(out=rows.rearrange("(a p) c -> p a c", p=P), in_=out_tile[:])
+
+        codes = new_codes()
+        for j in range(CHUNKS):
+            x_tile = first_x if j == 0 else load_chunk(j)
+            quantise_chunk(x_tile, codes[0], codes[1], slice(j * CHUNK, (j + 1) * CHUNK))
+
+        waiting = None
+        for n in range(BATCH):
+            next_codes = new_codes() if n + 1 < BATCH else None
+            out_tile = out_pool.tile([P, OUT_COLS // P, OUT_CH], F32, tag="out")
+            for v in range(BRANCHES):
+                pooled_by_group = []
+                for g in range(GROUPS):
+                    early, late = multiply(codes[0], codes[1], v, g)
+                    pooled_by_group.append(branch(early, late, v, g))
+                if next_codes is not None and v < CHUNKS:
+                    x_tile = load_chunk((n + 1) * CHUNKS + v)
+                    quantise_chunk(x_tile, next_codes[0], next_codes[1], slice(v * CHUNK, (v + 1) * CHUNK))
+                if waiting is not None:
+                    emit(waiting[0], waiting[1], waiting[2])
+                    if waiting[2] == BRANCHES - 1:
+                        store(waiting[0], waiting[3])
+                waiting = (out_tile, pooled_by_group, v, n)
+            codes = next_codes
+        emit(waiting[0], waiting[1], waiting[2])
+        store(waiting[0], waiting[3])

@@ -24,7 +24,9 @@ BANK = 512
 CHUNK = 2 * P
 CHUNKS = COLS // CHUNK
 OUT_COLS = COLS // 2
-OUT_CH = GROUPS * BRANCHES * CB
+BRANCH_ORDER = (1, 0, 2, 4, 3)
+LOAD_AHEAD = 2
+EMIT_LAG = 3
 
 FLOPS = 2 * BATCH * COLS * GROUPS * K * BRANCHES * CB
 
@@ -36,12 +38,12 @@ def tile_timeception_pa_t_e_kernel(tc, x, w_words, w_scales, b, dw, bn, out):
 
     with ExitStack() as ctx:
         const = ctx.enter_context(tc.tile_pool(name="const", bufs=1))
-        x_pool = ctx.enter_context(tc.tile_pool(name="x", bufs=6))
+        x_pool = ctx.enter_context(tc.tile_pool(name="x", bufs=LOAD_AHEAD + 2))
         grouped_pool = ctx.enter_context(tc.tile_pool(name="grouped", bufs=4))
         codes_pool = ctx.enter_context(tc.tile_pool(name="codes", bufs=2))
         work = ctx.enter_context(tc.tile_pool(name="work", bufs=4))
-        pooled_pool = ctx.enter_context(tc.tile_pool(name="pooled", bufs=6))
-        out_pool = ctx.enter_context(tc.tile_pool(name="outp", bufs=2))
+        pooled_pool = ctx.enter_context(tc.tile_pool(name="pooled", bufs=8))
+        out_pool = ctx.enter_context(tc.tile_pool(name="outp", bufs=4))
         flip_psum = ctx.enter_context(tc.psum_pool(name="flip", bufs=4))
         acc_psum = ctx.enter_context(tc.psum_pool(name="acc", bufs=4))
 
@@ -51,7 +53,9 @@ def tile_timeception_pa_t_e_kernel(tc, x, w_words, w_scales, b, dw, bn, out):
             nc.sync.dma_start(out=x_tile[:], in_=rows.rearrange("(a p) c -> p a c", p=P))
             return x_tile
 
-        first_x = load_chunk(0)
+        x_tiles = {}
+        for chunk in range(LOAD_AHEAD):
+            x_tiles[chunk] = load_chunk(chunk)
 
         w_codes = const.tile([P, BRANCHES * X_PASSES, CB], U32, align_bytes=64)
         w_planes = const.tile([P, BRANCHES * X_PASSES, CB], U8, align_bytes=64)
@@ -111,8 +115,8 @@ def tile_timeception_pa_t_e_kernel(tc, x, w_words, w_scales, b, dw, bn, out):
         nc.vector.tensor_add(out=c_last[:], in0=c_inner[:], in1=tap_bias[:, :, 0, :])
         nc.vector.tensor_add(out=c_inner[:], in0=c_first[:], in1=tap_bias[:, :, 0, :])
 
-        def quantise_chunk(x_tile, x_codes, x_planes, cols):
-            for c in range(X_PASSES):
+        def quantise(x_tile, x_codes, x_planes, cols, passes):
+            for c in passes:
                 flipped = flip_psum.tile([P, 2, 2, P], F32, tag="flip")
                 for a in range(2):
                     words = x_tile[:, a, :].bitcast(F32)
@@ -171,7 +175,7 @@ def tile_timeception_pa_t_e_kernel(tc, x, w_words, w_scales, b, dw, bn, out):
                 s = PIXELS
                 nc.vector.tensor_tensor(out=u[:, 0 : BANK - s], in0=early[:, s:BANK], in1=u[:, 0 : BANK - s], op=ALU.max)
                 nc.vector.tensor_tensor(out=u[:, BANK - s : COLS - s], in0=late[:], in1=u[:, BANK - s : COLS - s], op=ALU.max)
-                affine(u[:], u[:], mul, add)
+                nc.gpsimd.tensor_scalar(out=u[:], in0=u[:], scalar1=mul, scalar2=add, op0=ALU.mult, op1=ALU.add)
             else:
                 i = v - 1
                 s = v * PIXELS
@@ -180,9 +184,9 @@ def tile_timeception_pa_t_e_kernel(tc, x, w_words, w_scales, b, dw, bn, out):
                 affine(u[:, s:BANK], early[:, s:BANK], centre, c_inner[:, i, g : g + 1])
                 affine(u[:, BANK : COLS - s], late[:, 0 : BANK - s], centre, c_inner[:, i, g : g + 1])
                 affine(u[:, COLS - s : COLS], late[:, BANK - s : BANK], centre, c_last[:, i, g : g + 1])
+                add_tap(u[:, 0 : BANK - s], early[:, s:BANK], after)
                 add_tap(u[:, s : s + BANK], early[:], before)
                 add_tap(u[:, s + BANK : COLS], late[:, 0 : BANK - s], before)
-                add_tap(u[:, 0 : BANK - s], early[:, s:BANK], after)
                 add_tap(u[:, BANK - s : COLS - s], late[:], after)
             pooled = pooled_pool.tile([P, OUT_COLS], F32, tag="pooled")
             pairs = u[:].rearrange("p (t two q) -> p t two q", two=2, q=PIXELS)
@@ -191,46 +195,51 @@ def tile_timeception_pa_t_e_kernel(tc, x, w_words, w_scales, b, dw, bn, out):
             )
             return pooled
 
-        def emit(out_tile, pooled_by_group, v):
-            for pair in range(OUT_COLS // CHUNK):
-                flipped = flip_psum.tile([P, 2, GROUPS, P], F32, tag="flip")
-                for a in range(2):
-                    first = (2 * pair + a) * P
-                    for g in range(GROUPS):
-                        nc.tensor.transpose(flipped[:, a, g, :], pooled_by_group[g][:, first : first + P], ident[:])
-                channels = out_tile[:, 2 * pair : 2 * pair + 2, v * GROUPS * CB : (v + 1) * GROUPS * CB]
-                nc.scalar.activation(
-                    out=channels.rearrange("p a (o g) -> p a o g", g=GROUPS),
-                    in_=flipped[:].rearrange("p a g o -> p a o g"),
-                    func=ACT.Relu,
-                )
+        def emit(pooled_by_group, n, v, pair):
+            flipped = flip_psum.tile([P, 2, GROUPS, P], F32, tag="flip")
+            for a in range(2):
+                first = (2 * pair + a) * P
+                for g in range(GROUPS):
+                    nc.tensor.transpose(flipped[:, a, g, :], pooled_by_group[g][:, first : first + P], ident[:])
+            out_tile = out_pool.tile([P, 2, GROUPS * CB], F32, tag="out")
+            nc.scalar.activation(
+                out=out_tile[:].rearrange("p a (o g) -> p a o g", g=GROUPS),
+                in_=flipped[:].rearrange("p a g o -> p a o g"),
+                func=ACT.Relu,
+            )
+            rows = out_rows[n * OUT_COLS + pair * CHUNK : n * OUT_COLS + (pair + 1) * CHUNK, :]
+            channels = rows[:, v * GROUPS * CB : (v + 1) * GROUPS * CB]
+            nc.sync.dma_start(out=channels.rearrange("(a p) c -> p a c", p=P), in_=out_tile[:])
 
-        def store(out_tile, n):
-            rows = out_rows[n * OUT_COLS : (n + 1) * OUT_COLS, :]
-            nc.sync.dma_start(out=rows.rearrange("(a p) c -> p a c", p=P), in_=out_tile[:])
+        def take_chunk(chunk):
+            if chunk + LOAD_AHEAD < BATCH * CHUNKS:
+                x_tiles[chunk + LOAD_AHEAD] = load_chunk(chunk + LOAD_AHEAD)
+            return x_tiles[chunk]
 
         codes = new_codes()
         for j in range(CHUNKS):
-            x_tile = first_x if j == 0 else load_chunk(j)
-            quantise_chunk(x_tile, codes[0], codes[1], slice(j * CHUNK, (j + 1) * CHUNK))
+            quantise(take_chunk(j), codes[0], codes[1], slice(j * CHUNK, (j + 1) * CHUNK), range(X_PASSES))
 
-        waiting = None
+        branches_done = []
+        unit = 0
         for n in range(BATCH):
             next_codes = new_codes() if n + 1 < BATCH else None
-            out_tile = out_pool.tile([P, OUT_COLS // P, OUT_CH], F32, tag="out")
-            for v in range(BRANCHES):
+            for place, v in enumerate(BRANCH_ORDER):
                 pooled_by_group = []
+                branches_done.append((pooled_by_group, n, v))
+                if next_codes is not None and place < CHUNKS:
+                    x_tile = take_chunk((n + 1) * CHUNKS + place)
                 for g in range(GROUPS):
                     early, late = multiply(codes[0], codes[1], v, g)
                     pooled_by_group.append(branch(early, late, v, g))
-                if next_codes is not None and v < CHUNKS:
-                    x_tile = load_chunk((n + 1) * CHUNKS + v)
-                    quantise_chunk(x_tile, next_codes[0], next_codes[1], slice(v * CHUNK, (v + 1) * CHUNK))
-                if waiting is not None:
-                    emit(waiting[0], waiting[1], waiting[2])
-                    if waiting[2] == BRANCHES - 1:
-                        store(waiting[0], waiting[3])
-                waiting = (out_tile, pooled_by_group, v, n)
+                    if next_codes is not None and place < CHUNKS:
+                        cols = slice(place * CHUNK, (place + 1) * CHUNK)
+                        quantise(x_tile, next_codes[0], next_codes[1], cols, range(PASSES * g, PASSES * (g + 1)))
+                    if unit >= EMIT_LAG:
+                        done = branches_done[(unit - EMIT_LAG) // 2]
+                        emit(done[0], done[1], done[2], (unit - EMIT_LAG) % 2)
+                    unit += 1
             codes = next_codes
-        emit(waiting[0], waiting[1], waiting[2])
-        store(waiting[0], waiting[3])
+        for late_unit in range(unit, unit + EMIT_LAG):
+            done = branches_done[(late_unit - EMIT_LAG) // 2]
+            emit(done[0], done[1], done[2], (late_unit - EMIT_LAG) % 2)

@@ -18,15 +18,19 @@ GROUPS, K, CB, BRANCHES = 2, 1024, 128, 5
 EPS = 1e-3
 K_PASS = 4 * P
 PASSES = K // K_PASS
-X_PASSES = GROUPS * PASSES
 COLS = TIME * PIXELS
 BANK = 512
 CHUNK = 2 * P
 CHUNKS = COLS // CHUNK
 OUT_COLS = COLS // 2
+SLICES = BATCH * GROUPS
+LOADS = SLICES * CHUNKS
+FLIPS = LOADS * PASSES
 BRANCH_ORDER = (1, 0, 2, 4, 3)
-LOAD_AHEAD = 2
-EMIT_LAG = 3
+FIRST_ORDER = (0, 1, 4, 2, 3)
+LAST_ORDER = (1, 2, 3, 4, 0)
+LOAD_AHEAD = 4
+FLIPS_A_UNIT = 2
 
 FLOPS = 2 * BATCH * COLS * GROUPS * K * BRANCHES * CB
 
@@ -38,40 +42,53 @@ def tile_timeception_pa_t_e_kernel(tc, x, w_words, w_scales, b, dw, bn, out):
 
     with ExitStack() as ctx:
         const = ctx.enter_context(tc.tile_pool(name="const", bufs=1))
-        x_pool = ctx.enter_context(tc.tile_pool(name="x", bufs=LOAD_AHEAD + 2))
-        grouped_pool = ctx.enter_context(tc.tile_pool(name="grouped", bufs=4))
-        codes_pool = ctx.enter_context(tc.tile_pool(name="codes", bufs=2))
+        x_pool = ctx.enter_context(tc.tile_pool(name="x", bufs=LOAD_AHEAD + 3))
+        grouped_pool = ctx.enter_context(tc.tile_pool(name="grouped", bufs=6))
+        codes_pool = ctx.enter_context(tc.tile_pool(name="codes", bufs=4))
         work = ctx.enter_context(tc.tile_pool(name="work", bufs=4))
-        pooled_pool = ctx.enter_context(tc.tile_pool(name="pooled", bufs=8))
+        pooled_pool = ctx.enter_context(tc.tile_pool(name="pooled", bufs=20))
         out_pool = ctx.enter_context(tc.tile_pool(name="outp", bufs=4))
         flip_psum = ctx.enter_context(tc.psum_pool(name="flip", bufs=4))
         acc_psum = ctx.enter_context(tc.psum_pool(name="acc", bufs=4))
 
-        def load_chunk(chunk):
-            x_tile = x_pool.tile([P, 2, GROUPS * K], BF16, tag="x")
-            rows = x_rows[chunk * CHUNK : (chunk + 1) * CHUNK, :]
-            nc.sync.dma_start(out=x_tile[:], in_=rows.rearrange("(a p) c -> p a c", p=P))
-            return x_tile
-
         x_tiles = {}
-        for chunk in range(LOAD_AHEAD):
-            x_tiles[chunk] = load_chunk(chunk)
 
-        w_codes = const.tile([P, BRANCHES * X_PASSES, CB], U32, align_bytes=64)
-        w_planes = const.tile([P, BRANCHES * X_PASSES, CB], U8, align_bytes=64)
+        def load(index):
+            if index >= LOADS:
+                return
+            n, g, chunk = index // (GROUPS * CHUNKS), (index // CHUNKS) % GROUPS, index % CHUNKS
+            x_tile = x_pool.tile([P, 2, K], BF16, tag="x")
+            first = (n * CHUNKS + chunk) * CHUNK
+            rows = x_rows[first : first + CHUNK, g * K : (g + 1) * K]
+            nc.sync.dma_start(out=x_tile[:], in_=rows.rearrange("(a p) c -> p a c", p=P))
+            x_tiles[index] = x_tile
+
+        w_codes = const.tile([P, BRANCHES * GROUPS * PASSES, CB], U32, align_bytes=64)
+        w_planes = const.tile([P, BRANCHES * GROUPS * PASSES, CB], U8, align_bytes=64)
         nc.vector.memset(w_planes[:].bitcast(I32), 0)
+        w_words_i32 = w_words.rearrange("e p o t -> e p (o t)").bitcast(I32)
+
+        def load_codes(g):
+            for kp in range(PASSES):
+                first = g * PASSES + kp
+                step = GROUPS * PASSES
+                nc.sync.dma_start(
+                    out=w_codes[:, first : BRANCHES * step : step, :].bitcast(I32),
+                    in_=w_words_i32[first : BRANCHES * step : step].rearrange("e p o -> p e o"),
+                )
+
+        load(0)
+        load(1)
         for quad in range(4):
             nc.sync.dma_start(
                 out=w_planes[32 * quad : 32 * quad + 4].bitcast(I32),
                 in_=w_scales[:, 4 * quad : 4 * quad + 4, :].bitcast(I32).rearrange("e r o -> r e o"),
             )
-        nc.sync.dma_start(
-            out=w_codes[:].bitcast(I32),
-            in_=w_words.rearrange("e p o t -> e p (o t)").bitcast(I32).rearrange("e p o -> p e o"),
-        )
+        load_codes(0)
+        load(2)
+        load(3)
+        load_codes(1)
 
-        ident = const.tile([P, P], F32)
-        make_identity(nc, ident[:])
         n_b, n_dw, n_bn = BRANCHES * GROUPS, 3 * 3 * GROUPS, BRANCHES * 4 * GROUPS
         rows_bf = const.tile([P, CB], BF16)
         nc.vector.memset(rows_bf[:], 0.0)
@@ -80,6 +97,61 @@ def tile_timeception_pa_t_e_kernel(tc, x, w_words, w_scales, b, dw, bn, out):
         nc.scalar.dma_start(
             out=rows_bf[n_b + n_dw : n_b + n_dw + n_bn, :], in_=bn.rearrange("v j g o -> (v j g) o")
         )
+        warm = const.tile([P, 1], F32)
+        nc.vector.memset(warm[:], 1.0)
+        nc.scalar.activation(out=warm[:], in_=warm[:], func=ACT.Sqrt)
+        ident = const.tile([P, P], F32)
+        make_identity(nc, ident[:])
+
+        codes = {}
+
+        def flip(index, engine):
+            x_tile, kp = x_tiles[index // PASSES], index % PASSES
+            if index % (CHUNKS * PASSES) == 0:
+                x_codes = codes_pool.tile([P, PASSES, COLS], U32, align_bytes=64, tag="codes")
+                x_planes = codes_pool.tile([P, PASSES, COLS], U8, align_bytes=64, tag="planes")
+                codes[index // (CHUNKS * PASSES)] = (x_codes, x_planes)
+            flipped = flip_psum.tile([P, 2, 2, P], F32, tag="flip")
+            for a in range(2):
+                words = x_tile[:, a, :].bitcast(F32)
+                for u in range(2):
+                    nc.tensor.transpose(flipped[:, a, u, :], words[:, 256 * kp + u : 256 * (kp + 1) : 2], ident[:])
+            grouped = grouped_pool.tile([P, 4 * CHUNK], BF16, align_bytes=64, tag="grouped")
+            dst = grouped[:].bitcast(F32).rearrange("p (a r u) -> p a r u", a=2, u=2)
+            src = flipped[:].rearrange("p a u r -> p a r u")
+            if engine == "scalar":
+                nc.scalar.copy(out=dst, in_=src)
+            else:
+                nc.vector.tensor_copy(out=dst, in_=src)
+            return index, grouped
+
+        def quantise(index, grouped):
+            x_codes, x_planes = codes[index // (CHUNKS * PASSES)]
+            chunk, kp = (index // PASSES) % CHUNKS, index % PASSES
+            cols = slice(chunk * CHUNK, (chunk + 1) * CHUNK)
+            nc.vector.quantize_mx(out=x_codes[:, kp, cols].bitcast(FP8X4), scales=x_planes[:, kp, cols], in_=grouped[:])
+
+        def multiply(n, v, g, half):
+            x_codes, x_planes = codes[n * GROUPS + g]
+            acc = acc_psum.tile([P, BANK], F32, tag="acc")
+            cols = slice(half * BANK, (half + 1) * BANK)
+            for kp in range(PASSES):
+                e = (v * GROUPS + g) * PASSES + kp
+                nc.tensor.matmul_mx(
+                    out=acc[:],
+                    lhsT=w_codes[:, e, :].bitcast(FP8X4),
+                    lhsT_scale=w_planes[:, e, :],
+                    rhs=x_codes[:, kp, cols].bitcast(FP8X4),
+                    rhs_scale=x_planes[:, kp, cols],
+                    start=(kp == 0),
+                    stop=(kp == PASSES - 1),
+                )
+            return acc
+
+        for index in range(4):
+            quantise(*flip(index, ("scalar", "vector")[index % 2]))
+        first_early = multiply(0, FIRST_ORDER[0], 0, 0)
+
         rows_f32 = const.tile([P, CB], F32)
         nc.vector.tensor_copy(out=rows_f32[:], in_=rows_bf[:])
         params_ps = flip_psum.tile([P, BANK], F32, tag="flip")
@@ -115,47 +187,8 @@ def tile_timeception_pa_t_e_kernel(tc, x, w_words, w_scales, b, dw, bn, out):
         nc.vector.tensor_add(out=c_last[:], in0=c_inner[:], in1=tap_bias[:, :, 0, :])
         nc.vector.tensor_add(out=c_inner[:], in0=c_first[:], in1=tap_bias[:, :, 0, :])
 
-        def quantise(x_tile, x_codes, x_planes, cols, passes):
-            for c in passes:
-                flipped = flip_psum.tile([P, 2, 2, P], F32, tag="flip")
-                for a in range(2):
-                    words = x_tile[:, a, :].bitcast(F32)
-                    for u in range(2):
-                        nc.tensor.transpose(
-                            flipped[:, a, u, :], words[:, 256 * c + u : 256 * (c + 1) : 2], ident[:]
-                        )
-                grouped = grouped_pool.tile([P, 4 * CHUNK], BF16, align_bytes=64)
-                nc.scalar.copy(
-                    out=grouped[:].bitcast(F32).rearrange("p (a r u) -> p a r u", a=2, u=2),
-                    in_=flipped[:].rearrange("p a u r -> p a r u"),
-                )
-                nc.vector.quantize_mx(
-                    out=x_codes[:, c, cols].bitcast(FP8X4), scales=x_planes[:, c, cols], in_=grouped[:]
-                )
-
-        def new_codes():
-            x_codes = codes_pool.tile([P, X_PASSES, COLS], U32, align_bytes=64, tag="codes")
-            x_planes = codes_pool.tile([P, X_PASSES, COLS], U8, align_bytes=64, tag="planes")
-            return x_codes, x_planes
-
-        def multiply(x_codes, x_planes, v, g):
-            early = acc_psum.tile([P, BANK], F32, tag="acc")
-            late = acc_psum.tile([P, BANK], F32, tag="acc")
-            for half, acc in enumerate((early, late)):
-                cols = slice(half * BANK, (half + 1) * BANK)
-                for kp in range(PASSES):
-                    e = (v * GROUPS + g) * PASSES + kp
-                    c = g * PASSES + kp
-                    nc.tensor.matmul_mx(
-                        out=acc[:],
-                        lhsT=w_codes[:, e, :].bitcast(FP8X4),
-                        lhsT_scale=w_planes[:, e, :],
-                        rhs=x_codes[:, c, cols].bitcast(FP8X4),
-                        rhs_scale=x_planes[:, c, cols],
-                        start=(kp == 0),
-                        stop=(kp == PASSES - 1),
-                    )
-            return early, late
+        for index in range(4, 8):
+            quantise(*flip(index, ("scalar", "vector")[index % 2]))
 
         def affine(dst, src, mul, add):
             nc.scalar.activation(out=dst, in_=src, func=ACT.Identity, scale=mul, bias=add)
@@ -163,31 +196,43 @@ def tile_timeception_pa_t_e_kernel(tc, x, w_words, w_scales, b, dw, bn, out):
         def add_tap(dst, src, tap):
             nc.vector.scalar_tensor_tensor(out=dst, in0=src, scalar=tap, in1=dst, op0=ALU.mult, op1=ALU.add)
 
-        def branch(early, late, v, g):
+        def start_branch(early, late, v, g):
             u = work.tile([P, COLS], F32, tag="u")
             mul, add = scale[:, v, g : g + 1], offset[:, v, g : g + 1]
             if v == 0:
                 affine(u[:, 0:BANK], early[:], mul, add)
                 affine(u[:, BANK:COLS], late[:], mul, add)
-            elif v == 4:
+                return u, []
+            if v == 4:
                 nc.scalar.copy(out=u[:, 0:BANK], in_=early[:])
                 nc.scalar.copy(out=u[:, BANK:COLS], in_=late[:])
                 s = PIXELS
-                nc.vector.tensor_tensor(out=u[:, 0 : BANK - s], in0=early[:, s:BANK], in1=u[:, 0 : BANK - s], op=ALU.max)
-                nc.vector.tensor_tensor(out=u[:, BANK - s : COLS - s], in0=late[:], in1=u[:, BANK - s : COLS - s], op=ALU.max)
-                nc.gpsimd.tensor_scalar(out=u[:], in0=u[:], scalar1=mul, scalar2=add, op0=ALU.mult, op1=ALU.add)
-            else:
-                i = v - 1
-                s = v * PIXELS
-                before, centre, after = [s_taps[:, i, k, g : g + 1] for k in range(3)]
-                affine(u[:, 0:s], early[:, 0:s], centre, c_first[:, i, g : g + 1])
-                affine(u[:, s:BANK], early[:, s:BANK], centre, c_inner[:, i, g : g + 1])
-                affine(u[:, BANK : COLS - s], late[:, 0 : BANK - s], centre, c_inner[:, i, g : g + 1])
-                affine(u[:, COLS - s : COLS], late[:, BANK - s : BANK], centre, c_last[:, i, g : g + 1])
-                add_tap(u[:, 0 : BANK - s], early[:, s:BANK], after)
-                add_tap(u[:, s : s + BANK], early[:], before)
-                add_tap(u[:, s + BANK : COLS], late[:, 0 : BANK - s], before)
-                add_tap(u[:, BANK - s : COLS - s], late[:], after)
+                return u, [
+                    lambda: nc.vector.tensor_tensor(
+                        out=u[:, 0 : BANK - s], in0=early[:, s:BANK], in1=u[:, 0 : BANK - s], op=ALU.max
+                    ),
+                    lambda: nc.vector.tensor_tensor(
+                        out=u[:, BANK - s : COLS - s], in0=late[:], in1=u[:, BANK - s : COLS - s], op=ALU.max
+                    ),
+                    lambda: nc.gpsimd.tensor_scalar(
+                        out=u[:], in0=u[:], scalar1=mul, scalar2=add, op0=ALU.mult, op1=ALU.add
+                    ),
+                ]
+            i = v - 1
+            s = v * PIXELS
+            before, centre, after = [s_taps[:, i, k, g : g + 1] for k in range(3)]
+            affine(u[:, 0:s], early[:, 0:s], centre, c_first[:, i, g : g + 1])
+            affine(u[:, s:BANK], early[:, s:BANK], centre, c_inner[:, i, g : g + 1])
+            affine(u[:, BANK : COLS - s], late[:, 0 : BANK - s], centre, c_inner[:, i, g : g + 1])
+            affine(u[:, COLS - s : COLS], late[:, BANK - s : BANK], centre, c_last[:, i, g : g + 1])
+            return u, [
+                lambda: add_tap(u[:, 0 : BANK - s], early[:, s:BANK], after),
+                lambda: add_tap(u[:, s + BANK : COLS], late[:, 0 : BANK - s], before),
+                lambda: add_tap(u[:, s : s + BANK], early[:], before),
+                lambda: add_tap(u[:, BANK - s : COLS - s], late[:], after),
+            ]
+
+        def pool(u):
             pooled = pooled_pool.tile([P, OUT_COLS], F32, tag="pooled")
             pairs = u[:].rearrange("p (t two q) -> p t two q", two=2, q=PIXELS)
             nc.vector.tensor_tensor(
@@ -211,35 +256,60 @@ def tile_timeception_pa_t_e_kernel(tc, x, w_words, w_scales, b, dw, bn, out):
             channels = rows[:, v * GROUPS * CB : (v + 1) * GROUPS * CB]
             nc.sync.dma_start(out=channels.rearrange("(a p) c -> p a c", p=P), in_=out_tile[:])
 
-        def take_chunk(chunk):
-            if chunk + LOAD_AHEAD < BATCH * CHUNKS:
-                x_tiles[chunk + LOAD_AHEAD] = load_chunk(chunk + LOAD_AHEAD)
-            return x_tiles[chunk]
+        units = []
+        for n in range(BATCH - 1):
+            for g in range(GROUPS):
+                units.extend([(n, v, g) for v in (FIRST_ORDER if n + g == 0 else BRANCH_ORDER)])
+        units.extend([(BATCH - 1, v, g) for v in LAST_ORDER for g in range(GROUPS)])
 
-        codes = new_codes()
-        for j in range(CHUNKS):
-            quantise(take_chunk(j), codes[0], codes[1], slice(j * CHUNK, (j + 1) * CHUNK), range(X_PASSES))
+        for index in range(4, 4 + LOAD_AHEAD):
+            load(index)
+        next_flip = 8
+        to_quantise = []
+        to_pool = None
+        pooled_tiles = {}
+        pooled_now = []
+        to_emit = []
+        emitted = 0
 
-        branches_done = []
-        unit = 0
-        for n in range(BATCH):
-            next_codes = new_codes() if n + 1 < BATCH else None
-            for place, v in enumerate(BRANCH_ORDER):
-                pooled_by_group = []
-                branches_done.append((pooled_by_group, n, v))
-                if next_codes is not None and place < CHUNKS:
-                    x_tile = take_chunk((n + 1) * CHUNKS + place)
-                for g in range(GROUPS):
-                    early, late = multiply(codes[0], codes[1], v, g)
-                    pooled_by_group.append(branch(early, late, v, g))
-                    if next_codes is not None and place < CHUNKS:
-                        cols = slice(place * CHUNK, (place + 1) * CHUNK)
-                        quantise(x_tile, next_codes[0], next_codes[1], cols, range(PASSES * g, PASSES * (g + 1)))
-                    if unit >= EMIT_LAG:
-                        done = branches_done[(unit - EMIT_LAG) // 2]
-                        emit(done[0], done[1], done[2], (unit - EMIT_LAG) % 2)
-                    unit += 1
-            codes = next_codes
-        for late_unit in range(unit, unit + EMIT_LAG):
-            done = branches_done[(late_unit - EMIT_LAG) // 2]
-            emit(done[0], done[1], done[2], (late_unit - EMIT_LAG) % 2)
+        def pool_last():
+            u, n, v, g = to_pool
+            pooled_tiles.setdefault((n, v), {})[g] = pool(u)
+            if len(pooled_tiles[(n, v)]) == GROUPS:
+                pooled_now.append((n, v))
+
+        for place, (n, v, g) in enumerate(units):
+            early = first_early if place == 0 else multiply(n, v, g, 0)
+            late = multiply(n, v, g, 1)
+            u, steps = start_branch(early, late, v, g)
+            copied = []
+            for turn in range(FLIPS_A_UNIT):
+                if next_flip < FLIPS:
+                    if next_flip % PASSES == 0:
+                        load(next_flip // PASSES + LOAD_AHEAD)
+                    copied.append(flip(next_flip, "scalar"))
+                    next_flip += 1
+            fillers = [] if to_pool is None else [pool_last]
+            fillers.extend([lambda item=item: quantise(*item) for item in to_quantise])
+            filled = 0
+            for number, step in enumerate(steps):
+                step()
+                if number >= 1 and filled < len(fillers):
+                    fillers[filled]()
+                    filled += 1
+            for filler in fillers[filled:]:
+                filler()
+            to_quantise = copied
+            to_pool = (u, n, v, g)
+            for turn in range(1 if next_flip < FLIPS else 2):
+                if emitted < len(to_emit):
+                    emit(*to_emit[emitted])
+                    emitted += 1
+            for key in pooled_now:
+                to_emit.extend([(pooled_tiles[key], key[0], key[1], pair) for pair in range(2)])
+            pooled_now.clear()
+        pool_last()
+        for key in pooled_now:
+            to_emit.extend([(pooled_tiles[key], key[0], key[1], pair) for pair in range(2)])
+        for item in to_emit[emitted:]:
+            emit(*item)

@@ -28,7 +28,7 @@ LOADS = SLICES * CHUNKS
 FLIPS = LOADS * PASSES
 BRANCH_ORDER = (1, 0, 2, 4, 3)
 FIRST_ORDER = (0, 1, 4, 2, 3)
-LAST_ORDER = (1, 2, 3, 4, 0)
+LAST_UNITS = ((4, 0), (1, 0), (4, 1), (1, 1), (2, 0), (2, 1), (3, 0), (3, 1), (0, 0), (0, 1))
 LOAD_AHEAD = 4
 FLIPS_A_UNIT = 2
 
@@ -260,7 +260,7 @@ def tile_timeception_pa_t_e_kernel(tc, x, w_words, w_scales, b, dw, bn, out):
         for n in range(BATCH - 1):
             for g in range(GROUPS):
                 units.extend([(n, v, g) for v in (FIRST_ORDER if n + g == 0 else BRANCH_ORDER)])
-        units.extend([(BATCH - 1, v, g) for v in LAST_ORDER for g in range(GROUPS)])
+        units.extend([(BATCH - 1, v, g) for v, g in LAST_UNITS])
 
         for index in range(4, 4 + LOAD_AHEAD):
             load(index)
@@ -278,6 +278,7 @@ def tile_timeception_pa_t_e_kernel(tc, x, w_words, w_scales, b, dw, bn, out):
             if len(pooled_tiles[(n, v)]) == GROUPS:
                 pooled_now.append((n, v))
 
+        ctx.enter_context(tc.manual_schedule(engines={mybir.EngineType.DVE}))
         for place, (n, v, g) in enumerate(units):
             early = first_early if place == 0 else multiply(n, v, g, 0)
             late = multiply(n, v, g, 1)
@@ -292,9 +293,14 @@ def tile_timeception_pa_t_e_kernel(tc, x, w_words, w_scales, b, dw, bn, out):
             fillers = [] if to_pool is None else [pool_last]
             fillers.extend([lambda item=item: quantise(*item) for item in to_quantise])
             filled = 0
+            if v == 4:
+                for filler in fillers:
+                    filler()
+                filled = len(fillers)
+            first_gap = 2 if to_pool is not None and to_pool[2] == 4 else 1
             for number, step in enumerate(steps):
                 step()
-                if number >= 1 and filled < len(fillers):
+                if number >= first_gap and filled < len(fillers):
                     fillers[filled]()
                     filled += 1
             for filler in fillers[filled:]:

@@ -25,11 +25,9 @@ CHUNKS = COLS // CHUNK
 OUT_COLS = COLS // 2
 SLICES = BATCH * GROUPS
 LOADS = SLICES * CHUNKS
-FLIPS = LOADS * PASSES
 BRANCH_ORDER = (1, 0, 2, 4, 3)
 FIRST_ORDER = (0, 1, 4, 2, 3)
 LAST_UNITS = ((4, 0), (1, 0), (4, 1), (1, 1), (2, 0), (2, 1), (3, 0), (3, 1), (0, 0), (0, 1))
-LOAD_AHEAD = 4
 FLIPS_A_UNIT = 2
 
 FLOPS = 2 * BATCH * COLS * GROUPS * K * BRANCHES * CB
@@ -42,14 +40,15 @@ def tile_timeception_pa_t_e_kernel(tc, x, w_words, w_scales, b, dw, bn, out):
 
     with ExitStack() as ctx:
         const = ctx.enter_context(tc.tile_pool(name="const", bufs=1))
-        x_pool = ctx.enter_context(tc.tile_pool(name="x", bufs=LOAD_AHEAD + 3))
-        grouped_pool = ctx.enter_context(tc.tile_pool(name="grouped", bufs=6))
+        x_pool = ctx.enter_context(tc.tile_pool(name="x", bufs=2 * CHUNKS + 1))
+        narrow_pool = ctx.enter_context(tc.tile_pool(name="narrow", bufs=4))
+        wide_pool = ctx.enter_context(tc.tile_pool(name="wide", bufs=3))
         codes_pool = ctx.enter_context(tc.tile_pool(name="codes", bufs=4))
-        work = ctx.enter_context(tc.tile_pool(name="work", bufs=4))
+        work = ctx.enter_context(tc.tile_pool(name="work", bufs=5))
         pooled_pool = ctx.enter_context(tc.tile_pool(name="pooled", bufs=20))
-        out_pool = ctx.enter_context(tc.tile_pool(name="outp", bufs=4))
-        flip_psum = ctx.enter_context(tc.psum_pool(name="flip", bufs=4))
-        acc_psum = ctx.enter_context(tc.psum_pool(name="acc", bufs=4))
+        out_pool = ctx.enter_context(tc.tile_pool(name="outp", bufs=6))
+        flip_psum = ctx.enter_context(tc.psum_pool(name="flip", bufs=3))
+        acc_psum = ctx.enter_context(tc.psum_pool(name="acc", bufs=5))
 
         x_tiles = {}
 
@@ -105,31 +104,33 @@ def tile_timeception_pa_t_e_kernel(tc, x, w_words, w_scales, b, dw, bn, out):
 
         codes = {}
 
-        def flip(index, engine):
-            x_tile, kp = x_tiles[index // PASSES], index % PASSES
-            if index % (CHUNKS * PASSES) == 0:
+        def flip(part, kp, chunk, grouped, engine):
+            x_tile = x_tiles[part * CHUNKS + chunk]
+            if part not in codes:
                 x_codes = codes_pool.tile([P, PASSES, COLS], U32, align_bytes=64, tag="codes")
                 x_planes = codes_pool.tile([P, PASSES, COLS], U8, align_bytes=64, tag="planes")
-                codes[index // (CHUNKS * PASSES)] = (x_codes, x_planes)
+                codes[part] = (x_codes, x_planes)
             flipped = flip_psum.tile([P, 2, 2, P], F32, tag="flip")
             for a in range(2):
                 words = x_tile[:, a, :].bitcast(F32)
                 for u in range(2):
                     nc.tensor.transpose(flipped[:, a, u, :], words[:, 256 * kp + u : 256 * (kp + 1) : 2], ident[:])
-            grouped = grouped_pool.tile([P, 4 * CHUNK], BF16, align_bytes=64, tag="grouped")
-            dst = grouped[:].bitcast(F32).rearrange("p (a r u) -> p a r u", a=2, u=2)
+            dst = grouped.bitcast(F32).rearrange("p (a r u) -> p a r u", a=2, u=2)
             src = flipped[:].rearrange("p a u r -> p a r u")
             if engine == "scalar":
                 nc.scalar.copy(out=dst, in_=src)
             else:
                 nc.vector.tensor_copy(out=dst, in_=src)
-            return index, grouped
 
-        def quantise(index, grouped):
-            x_codes, x_planes = codes[index // (CHUNKS * PASSES)]
-            chunk, kp = (index // PASSES) % CHUNKS, index % PASSES
-            cols = slice(chunk * CHUNK, (chunk + 1) * CHUNK)
-            nc.vector.quantize_mx(out=x_codes[:, kp, cols].bitcast(FP8X4), scales=x_planes[:, kp, cols], in_=grouped[:])
+        def quantise(part, kp, cols, grouped):
+            x_codes, x_planes = codes[part]
+            nc.vector.quantize_mx(out=x_codes[:, kp, cols].bitcast(FP8X4), scales=x_planes[:, kp, cols], in_=grouped)
+
+        def head_flip(index):
+            chunk, kp = index // PASSES, index % PASSES
+            narrow = narrow_pool.tile([P, 4 * CHUNK], BF16, align_bytes=64, tag="narrow")
+            flip(0, kp, chunk, narrow[:], ("scalar", "vector")[index % 2])
+            quantise(0, kp, slice(chunk * CHUNK, (chunk + 1) * CHUNK), narrow[:])
 
         def multiply(n, v, g, half):
             x_codes, x_planes = codes[n * GROUPS + g]
@@ -149,7 +150,7 @@ def tile_timeception_pa_t_e_kernel(tc, x, w_words, w_scales, b, dw, bn, out):
             return acc
 
         for index in range(4):
-            quantise(*flip(index, ("scalar", "vector")[index % 2]))
+            head_flip(index)
         first_early = multiply(0, FIRST_ORDER[0], 0, 0)
 
         rows_f32 = const.tile([P, CB], F32)
@@ -188,7 +189,7 @@ def tile_timeception_pa_t_e_kernel(tc, x, w_words, w_scales, b, dw, bn, out):
         nc.vector.tensor_add(out=c_inner[:], in0=c_first[:], in1=tap_bias[:, :, 0, :])
 
         for index in range(4, 8):
-            quantise(*flip(index, ("scalar", "vector")[index % 2]))
+            head_flip(index)
 
         def affine(dst, src, mul, add):
             nc.scalar.activation(out=dst, in_=src, func=ACT.Identity, scale=mul, bias=add)
@@ -226,10 +227,10 @@ def tile_timeception_pa_t_e_kernel(tc, x, w_words, w_scales, b, dw, bn, out):
             affine(u[:, BANK : COLS - s], late[:, 0 : BANK - s], centre, c_inner[:, i, g : g + 1])
             affine(u[:, COLS - s : COLS], late[:, BANK - s : BANK], centre, c_last[:, i, g : g + 1])
             return u, [
+                lambda: add_tap(u[:, BANK - s : COLS - s], late[:], after),
                 lambda: add_tap(u[:, 0 : BANK - s], early[:, s:BANK], after),
                 lambda: add_tap(u[:, s + BANK : COLS], late[:, 0 : BANK - s], before),
                 lambda: add_tap(u[:, s : s + BANK], early[:], before),
-                lambda: add_tap(u[:, BANK - s : COLS - s], late[:], after),
             ]
 
         def pool(u):
@@ -262,9 +263,11 @@ def tile_timeception_pa_t_e_kernel(tc, x, w_words, w_scales, b, dw, bn, out):
                 units.extend([(n, v, g) for v in (FIRST_ORDER if n + g == 0 else BRANCH_ORDER)])
         units.extend([(BATCH - 1, v, g) for v, g in LAST_UNITS])
 
-        for index in range(4, 4 + LOAD_AHEAD):
-            load(index)
-        next_flip = 8
+        for chunk in range(CHUNKS):
+            load(CHUNKS + chunk)
+        flips = [(part, kp, chunk) for part in range(1, SLICES) for kp in range(PASSES) for chunk in range(CHUNKS)]
+        flipped_so_far = 0
+        wide = None
         to_quantise = []
         to_pool = None
         pooled_tiles = {}
@@ -283,31 +286,29 @@ def tile_timeception_pa_t_e_kernel(tc, x, w_words, w_scales, b, dw, bn, out):
             early = first_early if place == 0 else multiply(n, v, g, 0)
             late = multiply(n, v, g, 1)
             u, steps = start_branch(early, late, v, g)
-            copied = []
-            for turn in range(FLIPS_A_UNIT):
-                if next_flip < FLIPS:
-                    if next_flip % PASSES == 0:
-                        load(next_flip // PASSES + LOAD_AHEAD)
-                    copied.append(flip(next_flip, "scalar"))
-                    next_flip += 1
-            fillers = [] if to_pool is None else [pool_last]
-            fillers.extend([lambda item=item: quantise(*item) for item in to_quantise])
-            filled = 0
+            filled = []
+            for part, kp, chunk in flips[flipped_so_far : flipped_so_far + FLIPS_A_UNIT]:
+                if kp == 0:
+                    load((part + 1) * CHUNKS + chunk)
+                if chunk == 0:
+                    wide = wide_pool.tile([P, 4 * COLS], BF16, align_bytes=64, tag="wide")
+                flip(part, kp, chunk, wide[:, 4 * CHUNK * chunk : 4 * CHUNK * (chunk + 1)], "scalar")
+                if chunk == CHUNKS - 1:
+                    filled.append((part, kp, slice(0, COLS), wide[:]))
+            flipped_so_far += FLIPS_A_UNIT
+            if v != 4:
+                for step in steps:
+                    step()
+            if to_pool is not None:
+                pool_last()
+            for item in to_quantise:
+                quantise(*item)
             if v == 4:
-                for filler in fillers:
-                    filler()
-                filled = len(fillers)
-            first_gap = 2 if to_pool is not None and to_pool[2] == 4 else 1
-            for number, step in enumerate(steps):
-                step()
-                if number >= first_gap and filled < len(fillers):
-                    fillers[filled]()
-                    filled += 1
-            for filler in fillers[filled:]:
-                filler()
-            to_quantise = copied
+                for step in steps:
+                    step()
+            to_quantise = filled
             to_pool = (u, n, v, g)
-            for turn in range(1 if next_flip < FLIPS else 2):
+            for turn in range(1 if flipped_so_far < len(flips) else 2):
                 if emitted < len(to_emit):
                     emit(*to_emit[emitted])
                     emitted += 1

@@ -28,7 +28,8 @@ LOADS = SLICES * CHUNKS
 BRANCH_ORDER = (1, 0, 2, 4, 3)
 FIRST_ORDER = (0, 1, 4, 2, 3)
 LAST_UNITS = ((4, 0), (1, 0), (4, 1), (1, 1), (2, 0), (2, 1), (3, 0), (3, 1), (0, 0), (0, 1))
-FLIPS_A_UNIT = 2
+TURNS_A_UNIT = 3
+QUANTISE_AHEAD = 2
 
 FLOPS = 2 * BATCH * COLS * GROUPS * K * BRANCHES * CB
 
@@ -42,8 +43,8 @@ def tile_timeception_pa_t_e_kernel(tc, x, w_words, w_scales, b, dw, bn, out):
         const = ctx.enter_context(tc.tile_pool(name="const", bufs=1))
         x_pool = ctx.enter_context(tc.tile_pool(name="x", bufs=2 * CHUNKS + 1))
         narrow_pool = ctx.enter_context(tc.tile_pool(name="narrow", bufs=4))
-        wide_pool = ctx.enter_context(tc.tile_pool(name="wide", bufs=3))
-        codes_pool = ctx.enter_context(tc.tile_pool(name="codes", bufs=4))
+        wide_pool = ctx.enter_context(tc.tile_pool(name="wide", bufs=4))
+        codes_pool = ctx.enter_context(tc.tile_pool(name="codes", bufs=5))
         work = ctx.enter_context(tc.tile_pool(name="work", bufs=5))
         pooled_pool = ctx.enter_context(tc.tile_pool(name="pooled", bufs=20))
         out_pool = ctx.enter_context(tc.tile_pool(name="outp", bufs=6))
@@ -227,10 +228,10 @@ def tile_timeception_pa_t_e_kernel(tc, x, w_words, w_scales, b, dw, bn, out):
             affine(u[:, BANK : COLS - s], late[:, 0 : BANK - s], centre, c_inner[:, i, g : g + 1])
             affine(u[:, COLS - s : COLS], late[:, BANK - s : BANK], centre, c_last[:, i, g : g + 1])
             return u, [
-                lambda: add_tap(u[:, BANK - s : COLS - s], late[:], after),
-                lambda: add_tap(u[:, 0 : BANK - s], early[:, s:BANK], after),
-                lambda: add_tap(u[:, s + BANK : COLS], late[:, 0 : BANK - s], before),
                 lambda: add_tap(u[:, s : s + BANK], early[:], before),
+                lambda: add_tap(u[:, s + BANK : COLS], late[:, 0 : BANK - s], before),
+                lambda: add_tap(u[:, 0 : BANK - s], early[:, s:BANK], after),
+                lambda: add_tap(u[:, BANK - s : COLS - s], late[:], after),
             ]
 
         def pool(u):
@@ -268,7 +269,12 @@ def tile_timeception_pa_t_e_kernel(tc, x, w_words, w_scales, b, dw, bn, out):
         flips = [(part, kp, chunk) for part in range(1, SLICES) for kp in range(PASSES) for chunk in range(CHUNKS)]
         flipped_so_far = 0
         wide = None
+        filled = []
         to_quantise = []
+        quantised = 0
+        first_use = {}
+        for place, (n, v, g) in enumerate(units):
+            first_use.setdefault(n * GROUPS + g, place)
         to_pool = None
         pooled_tiles = {}
         pooled_now = []
@@ -286,8 +292,8 @@ def tile_timeception_pa_t_e_kernel(tc, x, w_words, w_scales, b, dw, bn, out):
             early = first_early if place == 0 else multiply(n, v, g, 0)
             late = multiply(n, v, g, 1)
             u, steps = start_branch(early, late, v, g)
-            filled = []
-            for part, kp, chunk in flips[flipped_so_far : flipped_so_far + FLIPS_A_UNIT]:
+            emits = min(len(to_emit) - emitted, 1 if flipped_so_far < len(flips) else 2)
+            for part, kp, chunk in flips[flipped_so_far : flipped_so_far + TURNS_A_UNIT - emits]:
                 if kp == 0:
                     load((part + 1) * CHUNKS + chunk)
                 if chunk == 0:
@@ -295,23 +301,28 @@ def tile_timeception_pa_t_e_kernel(tc, x, w_words, w_scales, b, dw, bn, out):
                 flip(part, kp, chunk, wide[:, 4 * CHUNK * chunk : 4 * CHUNK * (chunk + 1)], "scalar")
                 if chunk == CHUNKS - 1:
                     filled.append((part, kp, slice(0, COLS), wide[:]))
-            flipped_so_far += FLIPS_A_UNIT
+            flipped_so_far += TURNS_A_UNIT - emits
             if v != 4:
                 for step in steps:
                     step()
             if to_pool is not None:
                 pool_last()
-            for item in to_quantise:
-                quantise(*item)
+            room = {0: 2, 4: 1}.get(v, 0)
+            while quantised < len(to_quantise) and (
+                room > 0 or first_use[to_quantise[quantised][0]] - QUANTISE_AHEAD <= place
+            ):
+                quantise(*to_quantise[quantised])
+                quantised += 1
+                room -= 1
             if v == 4:
                 for step in steps:
                     step()
-            to_quantise = filled
+            to_quantise.extend(filled)
+            filled.clear()
             to_pool = (u, n, v, g)
-            for turn in range(1 if flipped_so_far < len(flips) else 2):
-                if emitted < len(to_emit):
-                    emit(*to_emit[emitted])
-                    emitted += 1
+            for turn in range(emits):
+                emit(*to_emit[emitted])
+                emitted += 1
             for key in pooled_now:
                 to_emit.extend([(pooled_tiles[key], key[0], key[1], pair) for pair in range(2)])
             pooled_now.clear()

@@ -26,10 +26,12 @@ OUT_COLS = COLS // 2
 SLICES = BATCH * GROUPS
 LOADS = SLICES * CHUNKS
 BRANCH_ORDER = (1, 0, 2, 4, 3)
-FIRST_ORDER = (0, 1, 4, 2, 3)
+FIRST_ORDER = (1, 2, 3, 0, 4)
 LAST_UNITS = ((4, 0), (1, 0), (4, 1), (1, 1), (2, 0), (2, 1), (3, 0), (3, 1), (0, 0), (0, 1))
 TURNS_A_UNIT = 3
 QUANTISE_AHEAD = 2
+FIRST_FLIP_UNIT = 1
+EMIT_LAG = 2
 
 FLOPS = 2 * BATCH * COLS * GROUPS * K * BRANCHES * CB
 
@@ -68,14 +70,12 @@ def tile_timeception_pa_t_e_kernel(tc, x, w_words, w_scales, b, dw, bn, out):
         nc.vector.memset(w_planes[:].bitcast(I32), 0)
         w_words_i32 = w_words.rearrange("e p o t -> e p (o t)").bitcast(I32)
 
-        def load_codes(g):
-            for kp in range(PASSES):
-                first = g * PASSES + kp
-                step = GROUPS * PASSES
-                nc.sync.dma_start(
-                    out=w_codes[:, first : BRANCHES * step : step, :].bitcast(I32),
-                    in_=w_words_i32[first : BRANCHES * step : step].rearrange("e p o -> p e o"),
-                )
+        def load_codes(v, g):
+            first = (v * GROUPS + g) * PASSES
+            nc.sync.dma_start(
+                out=w_codes[:, first : first + PASSES, :].bitcast(I32),
+                in_=w_words_i32[first : first + PASSES].rearrange("e p o -> p e o"),
+            )
 
         load(0)
         load(1)
@@ -84,10 +84,11 @@ def tile_timeception_pa_t_e_kernel(tc, x, w_words, w_scales, b, dw, bn, out):
                 out=w_planes[32 * quad : 32 * quad + 4].bitcast(I32),
                 in_=w_scales[:, 4 * quad : 4 * quad + 4, :].bitcast(I32).rearrange("e r o -> r e o"),
             )
-        load_codes(0)
+        load_codes(FIRST_ORDER[0], 0)
         load(2)
         load(3)
-        load_codes(1)
+        for v in FIRST_ORDER[1:]:
+            load_codes(v, 0)
 
         n_b, n_dw, n_bn = BRANCHES * GROUPS, 3 * 3 * GROUPS, BRANCHES * 4 * GROUPS
         rows_bf = const.tile([P, CB], BF16)
@@ -234,12 +235,18 @@ def tile_timeception_pa_t_e_kernel(tc, x, w_words, w_scales, b, dw, bn, out):
                 lambda: add_tap(u[:, BANK - s : COLS - s], late[:], after),
             ]
 
-        def pool(u):
+        def pool(u, pieces):
             pooled = pooled_pool.tile([P, OUT_COLS], F32, tag="pooled")
             pairs = u[:].rearrange("p (t two q) -> p t two q", two=2, q=PIXELS)
-            nc.vector.tensor_tensor(
-                out=pooled[:].rearrange("p (t q) -> p t q", q=PIXELS), in0=pairs[:, :, 0, :], in1=pairs[:, :, 1, :], op=ALU.max
-            )
+            steps = TIME // 2 // pieces
+            for piece in range(pieces):
+                t = slice(piece * steps, (piece + 1) * steps)
+                nc.vector.tensor_tensor(
+                    out=pooled[:].rearrange("p (t q) -> p t q", q=PIXELS)[:, t, :],
+                    in0=pairs[:, t, 0, :],
+                    in1=pairs[:, t, 1, :],
+                    op=ALU.max,
+                )
             return pooled
 
         def emit(pooled_by_group, n, v, pair):
@@ -266,6 +273,8 @@ def tile_timeception_pa_t_e_kernel(tc, x, w_words, w_scales, b, dw, bn, out):
 
         for chunk in range(CHUNKS):
             load(CHUNKS + chunk)
+        for v in BRANCH_ORDER:
+            load_codes(v, 1)
         flips = [(part, kp, chunk) for part in range(1, SLICES) for kp in range(PASSES) for chunk in range(CHUNKS)]
         flipped_so_far = 0
         wide = None
@@ -281,19 +290,21 @@ def tile_timeception_pa_t_e_kernel(tc, x, w_words, w_scales, b, dw, bn, out):
         to_emit = []
         emitted = 0
 
-        def pool_last():
+        def pool_last(pieces=1):
             u, n, v, g = to_pool
-            pooled_tiles.setdefault((n, v), {})[g] = pool(u)
+            pooled_tiles.setdefault((n, v), {})[g] = pool(u, pieces)
             if len(pooled_tiles[(n, v)]) == GROUPS:
                 pooled_now.append((n, v))
 
-        ctx.enter_context(tc.manual_schedule(engines={mybir.EngineType.DVE}))
+        ctx.enter_context(tc.manual_schedule(engines={mybir.EngineType.PE, mybir.EngineType.Activation, mybir.EngineType.DVE}))
         for place, (n, v, g) in enumerate(units):
             early = first_early if place == 0 else multiply(n, v, g, 0)
             late = multiply(n, v, g, 1)
             u, steps = start_branch(early, late, v, g)
-            emits = min(len(to_emit) - emitted, 1 if flipped_so_far < len(flips) else 2)
-            for part, kp, chunk in flips[flipped_so_far : flipped_so_far + TURNS_A_UNIT - emits]:
+            waiting = len([item for item in to_emit[emitted:] if item[0] <= place])
+            emits = min(waiting, 1 if flipped_so_far < len(flips) else 2)
+            turns = 0 if place < FIRST_FLIP_UNIT else TURNS_A_UNIT - emits
+            for part, kp, chunk in flips[flipped_so_far : flipped_so_far + turns]:
                 if kp == 0:
                     load((part + 1) * CHUNKS + chunk)
                 if chunk == 0:
@@ -301,7 +312,7 @@ def tile_timeception_pa_t_e_kernel(tc, x, w_words, w_scales, b, dw, bn, out):
                 flip(part, kp, chunk, wide[:, 4 * CHUNK * chunk : 4 * CHUNK * (chunk + 1)], "scalar")
                 if chunk == CHUNKS - 1:
                     filled.append((part, kp, slice(0, COLS), wide[:]))
-            flipped_so_far += TURNS_A_UNIT - emits
+            flipped_so_far += turns
             if v != 4:
                 for step in steps:
                     step()
@@ -321,13 +332,13 @@ def tile_timeception_pa_t_e_kernel(tc, x, w_words, w_scales, b, dw, bn, out):
             filled.clear()
             to_pool = (u, n, v, g)
             for turn in range(emits):
-                emit(*to_emit[emitted])
+                emit(*to_emit[emitted][1])
                 emitted += 1
             for key in pooled_now:
-                to_emit.extend([(pooled_tiles[key], key[0], key[1], pair) for pair in range(2)])
+                to_emit.extend([(place + 1 + EMIT_LAG, (pooled_tiles[key], key[0], key[1], pair)) for pair in range(2)])
             pooled_now.clear()
-        pool_last()
+        pool_last(2)
         for key in pooled_now:
-            to_emit.extend([(pooled_tiles[key], key[0], key[1], pair) for pair in range(2)])
+            to_emit.extend([(0, (pooled_tiles[key], key[0], key[1], pair)) for pair in range(2)])
         for item in to_emit[emitted:]:
-            emit(*item)
+            emit(*item[1])

@@ -27,8 +27,8 @@ SLICES = BATCH * GROUPS
 LOADS = SLICES * CHUNKS
 BRANCH_ORDER = (1, 0, 2, 4, 3)
 FIRST_ORDER = (1, 2, 3, 0, 4)
-LAST_UNITS = ((4, 0), (1, 0), (4, 1), (1, 1), (2, 0), (2, 1), (3, 0), (3, 1), (0, 0), (0, 1))
-TURNS_A_UNIT = 3
+LAST_UNITS = ((4, 0), (1, 0), (4, 1), (1, 1), (0, 0), (2, 0), (0, 1), (2, 1), (3, 0), (3, 1))
+TURNS = {0: 3, 1: 2, 2: 3, 3: 3, 4: 3}
 QUANTISE_AHEAD = 2
 FIRST_FLIP_UNIT = 1
 EMIT_LAG = 2
@@ -131,7 +131,7 @@ def tile_timeception_pa_t_e_kernel(tc, x, w_words, w_scales, b, dw, bn, out):
         def head_flip(index):
             chunk, kp = index // PASSES, index % PASSES
             narrow = narrow_pool.tile([P, 4 * CHUNK], BF16, align_bytes=64, tag="narrow")
-            flip(0, kp, chunk, narrow[:], ("scalar", "vector")[index % 2])
+            flip(0, kp, chunk, narrow[:], "scalar")
             quantise(0, kp, slice(chunk * CHUNK, (chunk + 1) * CHUNK), narrow[:])
 
         def multiply(n, v, g, half):
@@ -207,15 +207,22 @@ def tile_timeception_pa_t_e_kernel(tc, x, w_words, w_scales, b, dw, bn, out):
                 affine(u[:, BANK:COLS], late[:], mul, add)
                 return u, []
             if v == 4:
-                nc.scalar.copy(out=u[:, 0:BANK], in_=early[:])
-                nc.scalar.copy(out=u[:, BANK:COLS], in_=late[:])
-                s = PIXELS
+                half = TIME // 4
+                u_pairs = u[:].rearrange("p (j two q) -> p j two q", two=2, q=PIXELS)
+                e_pairs = early[:].rearrange("p (j two q) -> p j two q", two=2, q=PIXELS)
+                l_pairs = late[:].rearrange("p (j two q) -> p j two q", two=2, q=PIXELS)
+                nc.scalar.copy(out=u_pairs[:, 0:half, 1, :], in_=e_pairs[:, :, 1, :])
+                nc.scalar.copy(out=u_pairs[:, half : 2 * half, 1, :], in_=l_pairs[:, :, 1, :])
+
+                def larger(dst, src, odd):
+                    nc.vector.tensor_tensor(out=dst, in0=src, in1=odd, op=ALU.max)
+
                 return u, [
-                    lambda: nc.vector.tensor_tensor(
-                        out=u[:, 0 : BANK - s], in0=early[:, s:BANK], in1=u[:, 0 : BANK - s], op=ALU.max
-                    ),
-                    lambda: nc.vector.tensor_tensor(
-                        out=u[:, BANK - s : COLS - s], in0=late[:], in1=u[:, BANK - s : COLS - s], op=ALU.max
+                    lambda: larger(u_pairs[:, 0:half, 0, :], e_pairs[:, :, 0, :], u_pairs[:, 0:half, 1, :]),
+                    lambda: larger(u_pairs[:, half : 2 * half, 0, :], l_pairs[:, :, 0, :], u_pairs[:, half : 2 * half, 1, :]),
+                    lambda: larger(u_pairs[:, 0 : half - 1, 1, :], e_pairs[:, 1:half, 0, :], u_pairs[:, 0 : half - 1, 1, :]),
+                    lambda: larger(
+                        u_pairs[:, half - 1 : 2 * half - 1, 1, :], l_pairs[:, :, 0, :], u_pairs[:, half - 1 : 2 * half - 1, 1, :]
                     ),
                     lambda: nc.gpsimd.tensor_scalar(
                         out=u[:], in0=u[:], scalar1=mul, scalar2=add, op0=ALU.mult, op1=ALU.add
@@ -303,7 +310,7 @@ def tile_timeception_pa_t_e_kernel(tc, x, w_words, w_scales, b, dw, bn, out):
             u, steps = start_branch(early, late, v, g)
             waiting = len([item for item in to_emit[emitted:] if item[0] <= place])
             emits = min(waiting, 1 if flipped_so_far < len(flips) else 2)
-            turns = 0 if place < FIRST_FLIP_UNIT else TURNS_A_UNIT - emits
+            turns = 0 if place < FIRST_FLIP_UNIT else TURNS[v] - emits
             for part, kp, chunk in flips[flipped_so_far : flipped_so_far + turns]:
                 if kp == 0:
                     load((part + 1) * CHUNKS + chunk)

@@ -207,22 +207,15 @@ def tile_timeception_pa_t_e_kernel(tc, x, w_words, w_scales, b, dw, bn, out):
                 affine(u[:, BANK:COLS], late[:], mul, add)
                 return u, []
             if v == 4:
-                half = TIME // 4
-                u_pairs = u[:].rearrange("p (j two q) -> p j two q", two=2, q=PIXELS)
-                e_pairs = early[:].rearrange("p (j two q) -> p j two q", two=2, q=PIXELS)
-                l_pairs = late[:].rearrange("p (j two q) -> p j two q", two=2, q=PIXELS)
-                nc.scalar.copy(out=u_pairs[:, 0:half, 1, :], in_=e_pairs[:, :, 1, :])
-                nc.scalar.copy(out=u_pairs[:, half : 2 * half, 1, :], in_=l_pairs[:, :, 1, :])
-
-                def larger(dst, src, odd):
-                    nc.vector.tensor_tensor(out=dst, in0=src, in1=odd, op=ALU.max)
-
+                nc.scalar.copy(out=u[:, 0:BANK], in_=early[:])
+                nc.scalar.copy(out=u[:, BANK:COLS], in_=late[:])
+                s = PIXELS
                 return u, [
-                    lambda: larger(u_pairs[:, 0:half, 0, :], e_pairs[:, :, 0, :], u_pairs[:, 0:half, 1, :]),
-                    lambda: larger(u_pairs[:, half : 2 * half, 0, :], l_pairs[:, :, 0, :], u_pairs[:, half : 2 * half, 1, :]),
-                    lambda: larger(u_pairs[:, 0 : half - 1, 1, :], e_pairs[:, 1:half, 0, :], u_pairs[:, 0 : half - 1, 1, :]),
-                    lambda: larger(
-                        u_pairs[:, half - 1 : 2 * half - 1, 1, :], l_pairs[:, :, 0, :], u_pairs[:, half - 1 : 2 * half - 1, 1, :]
+                    lambda: nc.vector.tensor_tensor(
+                        out=u[:, 0 : BANK - s], in0=early[:, s:BANK], in1=u[:, 0 : BANK - s], op=ALU.max
+                    ),
+                    lambda: nc.vector.tensor_tensor(
+                        out=u[:, BANK - s : COLS - s], in0=late[:], in1=u[:, BANK - s : COLS - s], op=ALU.max
                     ),
                     lambda: nc.gpsimd.tensor_scalar(
                         out=u[:], in0=u[:], scalar1=mul, scalar2=add, op0=ALU.mult, op1=ALU.add

@@ -26,11 +26,12 @@ OUT_COLS = COLS // 2
 SLICES = BATCH * GROUPS
 LOADS = SLICES * CHUNKS
 BRANCH_ORDER = (1, 0, 2, 4, 3)
-FIRST_ORDER = (1, 2, 3, 0, 4)
+CONVOLUTIONS = (1, 2, 3)
+FIRST_ORDER = CONVOLUTIONS + (0, 4)
 LAST_UNITS = ((4, 0), (1, 0), (4, 1), (1, 1), (0, 0), (2, 0), (0, 1), (2, 1), (3, 0), (3, 1))
-TURNS = {0: 3, 1: 2, 2: 3, 3: 3, 4: 3}
-QUANTISE_AHEAD = 2
-FIRST_FLIP_UNIT = 1
+TURNS = {0: 2, 1: 3, 2: 3, 3: 3, 4: 2}
+LEAD = 1
+QUANTISE_AHEAD = 4
 EMIT_LAG = 2
 
 FLOPS = 2 * BATCH * COLS * GROUPS * K * BRANCHES * CB
@@ -48,6 +49,7 @@ def tile_timeception_pa_t_e_kernel(tc, x, w_words, w_scales, b, dw, bn, out):
         wide_pool = ctx.enter_context(tc.tile_pool(name="wide", bufs=4))
         codes_pool = ctx.enter_context(tc.tile_pool(name="codes", bufs=5))
         work = ctx.enter_context(tc.tile_pool(name="work", bufs=5))
+        light_pool = ctx.enter_context(tc.tile_pool(name="light", bufs=3))
         pooled_pool = ctx.enter_context(tc.tile_pool(name="pooled", bufs=20))
         out_pool = ctx.enter_context(tc.tile_pool(name="outp", bufs=6))
         flip_psum = ctx.enter_context(tc.psum_pool(name="flip", bufs=3))
@@ -68,41 +70,41 @@ def tile_timeception_pa_t_e_kernel(tc, x, w_words, w_scales, b, dw, bn, out):
         w_codes = const.tile([P, BRANCHES * GROUPS * PASSES, CB], U32, align_bytes=64)
         w_planes = const.tile([P, BRANCHES * GROUPS * PASSES, CB], U8, align_bytes=64)
         nc.vector.memset(w_planes[:].bitcast(I32), 0)
-        w_words_i32 = w_words.rearrange("e p o t -> e p (o t)").bitcast(I32)
-
-        def load_codes(v, g):
-            first = (v * GROUPS + g) * PASSES
-            nc.sync.dma_start(
-                out=w_codes[:, first : first + PASSES, :].bitcast(I32),
-                in_=w_words_i32[first : first + PASSES].rearrange("e p o -> p e o"),
-            )
-
-        load(0)
-        load(1)
-        for quad in range(4):
+        def load_planes(quad):
             nc.sync.dma_start(
                 out=w_planes[32 * quad : 32 * quad + 4].bitcast(I32),
                 in_=w_scales[:, 4 * quad : 4 * quad + 4, :].bitcast(I32).rearrange("e r o -> r e o"),
             )
-        load_codes(FIRST_ORDER[0], 0)
-        load(2)
-        load(3)
-        for v in FIRST_ORDER[1:]:
-            load_codes(v, 0)
+
+        w_words_by_pass = w_words.rearrange("(v gk) p o t -> gk p v (o t)", gk=GROUPS * PASSES).bitcast(I32)
+        w_codes_by_pass = w_codes[:].rearrange("p (v gk) o -> p gk v o", gk=GROUPS * PASSES)
+
+        def load_codes(branches, g):
+            v = slice(branches[0], branches[-1] + 1)
+            for gk in range(g * PASSES, (g + 1) * PASSES):
+                nc.sync.dma_start(out=w_codes_by_pass[:, gk, v, :].bitcast(I32), in_=w_words_by_pass[gk, :, v, :])
 
         n_b, n_dw, n_bn = BRANCHES * GROUPS, 3 * 3 * GROUPS, BRANCHES * 4 * GROUPS
         rows_bf = const.tile([P, CB], BF16)
-        nc.vector.memset(rows_bf[:], 0.0)
-        nc.scalar.dma_start(out=rows_bf[0:n_b, :], in_=b.rearrange("v g o -> (v g) o"))
+        nc.gpsimd.memset(rows_bf[:], 0.0)
+        load(0)
+        load(1)
+        nc.scalar.dma_start(out=rows_bf[n_b + n_dw : n_b + n_dw + n_bn, :], in_=bn.rearrange("v j g o -> (v j g) o"))
         nc.scalar.dma_start(out=rows_bf[n_b : n_b + n_dw, :], in_=dw.rearrange("i k g o -> (i k g) o"))
-        nc.scalar.dma_start(
-            out=rows_bf[n_b + n_dw : n_b + n_dw + n_bn, :], in_=bn.rearrange("v j g o -> (v j g) o")
-        )
-        warm = const.tile([P, 1], F32)
-        nc.vector.memset(warm[:], 1.0)
-        nc.scalar.activation(out=warm[:], in_=warm[:], func=ACT.Sqrt)
+        nc.scalar.dma_start(out=rows_bf[0:n_b, :], in_=b.rearrange("v g o -> (v g) o"))
+        load_codes(CONVOLUTIONS, 0)
+        load(2)
+        for quad in range(4):
+            load_planes(quad)
+        load(3)
+        for v in FIRST_ORDER[len(CONVOLUTIONS) :]:
+            load_codes((v,), 0)
         ident = const.tile([P, P], F32)
         make_identity(nc, ident[:])
+
+        warm = const.tile([P, 1], F32)
+        nc.vector.memset(warm[:], 1.0)
+        nc.scalar.activation(out=warm[:], in_=warm[:], func=ACT.Abs_reciprocal_sqrt)
 
         codes = {}
 
@@ -132,7 +134,7 @@ def tile_timeception_pa_t_e_kernel(tc, x, w_words, w_scales, b, dw, bn, out):
             chunk, kp = index // PASSES, index % PASSES
             narrow = narrow_pool.tile([P, 4 * CHUNK], BF16, align_bytes=64, tag="narrow")
             flip(0, kp, chunk, narrow[:], "scalar")
-            quantise(0, kp, slice(chunk * CHUNK, (chunk + 1) * CHUNK), narrow[:])
+            return lambda: quantise(0, kp, slice(chunk * CHUNK, (chunk + 1) * CHUNK), narrow[:])
 
         def multiply(n, v, g, half):
             x_codes, x_planes = codes[n * GROUPS + g]
@@ -151,89 +153,137 @@ def tile_timeception_pa_t_e_kernel(tc, x, w_words, w_scales, b, dw, bn, out):
                 )
             return acc
 
-        for index in range(4):
-            head_flip(index)
-        first_early = multiply(0, FIRST_ORDER[0], 0, 0)
+        ctx.enter_context(tc.manual_schedule(engines={mybir.EngineType.PE, mybir.EngineType.Activation, mybir.EngineType.DVE}))
+        ident_bf = const.tile([P, P], BF16)
+        nc.vector.tensor_copy(out=ident_bf[:], in_=ident[:])
+        head_quantise = [head_flip(0), head_flip(1)]
+        turned = acc_psum.tile([P, BANK], F32, tag="acc")
+        nc.tensor.matmul(turned[:, 0:P], lhsT=rows_bf[:], rhs=ident_bf[:], start=True, stop=True)
 
-        rows_f32 = const.tile([P, CB], F32)
-        nc.vector.tensor_copy(out=rows_f32[:], in_=rows_bf[:])
-        params_ps = flip_psum.tile([P, BANK], F32, tag="flip")
-        nc.tensor.transpose(params_ps[:, 0:P], rows_f32[:], ident[:])
-        params = const.tile([P, P], F32)
-        nc.vector.tensor_copy(out=params[:], in_=params_ps[:, 0:P])
-        bias = params[:, 0:n_b].rearrange("p (v g) -> p v g", g=GROUPS)
-        taps = params[:, n_b : n_b + n_dw].rearrange("p (i k g) -> p i k g", k=3, g=GROUPS)
-        bn_p = params[:, n_b + n_dw : n_b + n_dw + n_bn].rearrange("p (v j g) -> p v j g", j=4, g=GROUPS)
-        gamma, beta, mean, var = bn_p[:, :, 0, :], bn_p[:, :, 1, :], bn_p[:, :, 2, :], bn_p[:, :, 3, :]
+        def views(columns):
+            bn_columns = columns[:, n_b + n_dw : n_b + n_dw + n_bn].rearrange("p (v j g) -> p v j g", j=4, g=GROUPS)
+            return (
+                columns[:, 0:n_b].rearrange("p (v g) -> p v g", g=GROUPS),
+                columns[:, n_b : n_b + n_dw].rearrange("p (i k g) -> p i k g", k=3, g=GROUPS),
+                [bn_columns[:, :, j, :] for j in range(4)],
+            )
 
+        bias, taps, (gamma, beta, mean, var) = views(turned)
         scale = const.tile([P, BRANCHES, GROUPS], F32)
-        nc.vector.tensor_scalar_add(out=scale[:], in0=var, scalar1=EPS)
-        nc.scalar.activation(out=scale[:], in_=scale[:], func=ACT.Sqrt)
-        nc.vector.reciprocal(out=scale[:], in_=scale[:])
-        nc.vector.tensor_mul(out=scale[:], in0=scale[:], in1=gamma)
-        shift = const.tile([P, BRANCHES, GROUPS], F32)
-        nc.vector.tensor_mul(out=shift[:], in0=scale[:], in1=mean)
-        nc.vector.tensor_sub(out=shift[:], in0=beta, in1=shift[:])
-        offset = const.tile([P, BRANCHES, GROUPS], F32)
-        nc.vector.tensor_mul(out=offset[:], in0=scale[:], in1=bias)
-        nc.vector.tensor_add(out=offset[:], in0=offset[:], in1=shift[:])
+        nc.scalar.activation(out=scale[:], in_=var, func=ACT.Abs_reciprocal_sqrt, bias=EPS)
+        params = const.tile([P, P], F32)
+        nc.scalar.copy(out=params[:], in_=turned[:, 0:P])
+        head_quantise.append(head_flip(2))
+        head_quantise.append(head_flip(3))
         conv_shape = [P, 3, 3, GROUPS]
+        shift = const.tile([P, BRANCHES, GROUPS], F32)
         s_taps = const.tile(conv_shape, F32)
-        nc.vector.tensor_mul(out=s_taps[:], in0=taps, in1=scale[:, 1:4, :].unsqueeze(2).to_broadcast(conv_shape))
         tap_bias = const.tile(conv_shape, F32)
-        nc.vector.tensor_mul(out=tap_bias[:], in0=s_taps[:], in1=bias[:, 1:4, :].unsqueeze(2).to_broadcast(conv_shape))
+        c_centre = const.tile([P, 3, GROUPS], F32)
         c_inner = const.tile([P, 3, GROUPS], F32)
-        nc.vector.tensor_add(out=c_inner[:], in0=shift[:, 1:4, :], in1=tap_bias[:, :, 1, :])
         c_first = const.tile([P, 3, GROUPS], F32)
-        nc.vector.tensor_add(out=c_first[:], in0=c_inner[:], in1=tap_bias[:, :, 2, :])
         c_last = const.tile([P, 3, GROUPS], F32)
-        nc.vector.tensor_add(out=c_last[:], in0=c_inner[:], in1=tap_bias[:, :, 0, :])
+        head_quantise[0]()
+        nc.vector.tensor_mul(out=scale[:], in0=scale[:], in1=gamma)
+        head_quantise[1]()
+        nc.vector.tensor_mul(out=s_taps[:], in0=scale[:, 1:4, :].unsqueeze(2).to_broadcast(conv_shape), in1=taps)
+        nc.vector.tensor_mul(out=shift[:], in0=scale[:], in1=mean)
+        nc.vector.tensor_mul(out=tap_bias[:], in0=s_taps[:], in1=bias[:, 1:4, :].unsqueeze(2).to_broadcast(conv_shape))
+        nc.vector.tensor_sub(out=shift[:], in0=beta, in1=shift[:])
+        nc.vector.tensor_add(out=c_centre[:], in0=shift[:, 1:4, :], in1=tap_bias[:, :, 1, :])
+        head_quantise[2]()
+        nc.vector.tensor_add(out=c_first[:], in0=c_centre[:], in1=tap_bias[:, :, 2, :])
+        nc.vector.tensor_add(out=c_last[:], in0=c_centre[:], in1=tap_bias[:, :, 0, :])
+        head_quantise[3]()
         nc.vector.tensor_add(out=c_inner[:], in0=c_first[:], in1=tap_bias[:, :, 0, :])
-
-        for index in range(4, 8):
-            head_flip(index)
+        bias, taps, (gamma, beta, mean, var) = views(params)
+        offset = const.tile([P, BRANCHES, GROUPS], F32)
+        nc.gpsimd.tensor_mul(out=offset[:], in0=scale[:], in1=bias)
+        nc.gpsimd.tensor_add(out=offset[:], in0=offset[:], in1=shift[:])
+        sign = const.tile([P, BRANCHES, GROUPS], F32)
+        nc.gpsimd.tensor_scalar(out=sign[:], in0=gamma, scalar1=0.0, scalar2=2.0, op0=ALU.is_ge, op1=ALU.mult)
+        nc.gpsimd.tensor_scalar(out=sign[:], in0=sign[:], scalar1=1.0, scalar2=-1.0, op0=ALU.mult, op1=ALU.add)
 
         def affine(dst, src, mul, add):
             nc.scalar.activation(out=dst, in_=src, func=ACT.Identity, scale=mul, bias=add)
 
+        def scaled_copy(dst, src, mul):
+            nc.scalar.activation(out=dst, in_=src, func=ACT.Copy, scale=mul)
+
+        def sttmax(dst, src, mul, other):
+            nc.vector.scalar_tensor_tensor(out=dst, in0=src, scalar=mul, in1=other, op0=ALU.mult, op1=ALU.max)
+
         def add_tap(dst, src, tap):
             nc.vector.scalar_tensor_tensor(out=dst, in0=src, scalar=tap, in1=dst, op0=ALU.mult, op1=ALU.add)
 
-        def start_branch(early, late, v, g):
+        def outer_taps(v, g):
+            return s_taps[:, v - 1, 0, g : g + 1], s_taps[:, v - 1, 2, g : g + 1], v * PIXELS
+
+        def centre_early(early, v, g):
             u = work.tile([P, COLS], F32, tag="u")
-            mul, add = scale[:, v, g : g + 1], offset[:, v, g : g + 1]
-            if v == 0:
-                affine(u[:, 0:BANK], early[:], mul, add)
-                affine(u[:, BANK:COLS], late[:], mul, add)
-                return u, []
-            if v == 4:
-                nc.scalar.copy(out=u[:, 0:BANK], in_=early[:])
-                nc.scalar.copy(out=u[:, BANK:COLS], in_=late[:])
-                s = PIXELS
-                return u, [
-                    lambda: nc.vector.tensor_tensor(
-                        out=u[:, 0 : BANK - s], in0=early[:, s:BANK], in1=u[:, 0 : BANK - s], op=ALU.max
-                    ),
-                    lambda: nc.vector.tensor_tensor(
-                        out=u[:, BANK - s : COLS - s], in0=late[:], in1=u[:, BANK - s : COLS - s], op=ALU.max
-                    ),
-                    lambda: nc.gpsimd.tensor_scalar(
-                        out=u[:], in0=u[:], scalar1=mul, scalar2=add, op0=ALU.mult, op1=ALU.add
-                    ),
-                ]
-            i = v - 1
-            s = v * PIXELS
-            before, centre, after = [s_taps[:, i, k, g : g + 1] for k in range(3)]
+            i, s = v - 1, v * PIXELS
+            centre = s_taps[:, i, 1, g : g + 1]
             affine(u[:, 0:s], early[:, 0:s], centre, c_first[:, i, g : g + 1])
             affine(u[:, s:BANK], early[:, s:BANK], centre, c_inner[:, i, g : g + 1])
+            return u
+
+        def centre_late(u, late, v, g):
+            i, s = v - 1, v * PIXELS
+            centre = s_taps[:, i, 1, g : g + 1]
             affine(u[:, BANK : COLS - s], late[:, 0 : BANK - s], centre, c_inner[:, i, g : g + 1])
             affine(u[:, COLS - s : COLS], late[:, BANK - s : BANK], centre, c_last[:, i, g : g + 1])
+
+        def finish_convolution(u, early, late, v, g):
+            centre_late(u, late, v, g)
+            before, after, s = outer_taps(v, g)
+            return [
+                lambda: add_tap(u[:, BANK : BANK + s], early[:, BANK - s : BANK], before),
+                lambda: add_tap(u[:, BANK + s : COLS], late[:, 0 : BANK - s], before),
+                lambda: add_tap(u[:, BANK - s : BANK], late[:, 0:s], after),
+                lambda: add_tap(u[:, BANK : COLS - s], late[:, s:BANK], after),
+            ]
+
+        def start_branch(early, late, v, g):
+            mul, add = scale[:, v, g : g + 1], offset[:, v, g : g + 1]
+            if v in (0, 4):
+                m = light_pool.tile([P, OUT_COLS], F32, tag="m")
+                pairs = [
+                    bank[:].rearrange("p (t two q) -> p t two q", two=2, q=PIXELS) for bank in (early, late)
+                ]
+                m_rows = m[:].rearrange("p (t q) -> p t q", q=PIXELS)
+                half_rows = [m_rows[:, 0 : TIME // 4, :], m_rows[:, TIME // 4 : TIME // 2, :]]
+            if v == 0:
+                for rows, pair in zip(half_rows, pairs):
+                    scaled_copy(rows, pair[:, :, 1, :], mul)
+                return m, [
+                    lambda: sttmax(half_rows[0], pairs[0][:, :, 0, :], mul, half_rows[0]),
+                    lambda: sttmax(half_rows[1], pairs[1][:, :, 0, :], mul, half_rows[1]),
+                ], lambda dst: nc.gpsimd.tensor_scalar(
+                    out=dst, in0=m[:], scalar1=1.0, scalar2=add, op0=ALU.mult, op1=ALU.add
+                )
+            if v == 4:
+                sgn = sign[:, v, g : g + 1]
+                s = PIXELS
+                scaled_copy(m_rows[:, 0 : TIME // 4 - 1, :], pairs[0][:, 1:, 0, :], sgn)
+                scaled_copy(m_rows[:, TIME // 4 - 1 : TIME // 2 - 1, :], pairs[1][:, :, 0, :], sgn)
+                scaled_copy(m[:, OUT_COLS - s : OUT_COLS], late[:, BANK - s : BANK], sgn)
+                return m, [
+                    lambda: sttmax(half_rows[0], pairs[0][:, :, 0, :], sgn, half_rows[0]),
+                    lambda: sttmax(half_rows[1], pairs[1][:, :, 0, :], sgn, half_rows[1]),
+                    lambda: sttmax(half_rows[0], half_rows[0], sgn, pairs[0][:, :, 1, :]),
+                    lambda: sttmax(half_rows[1], half_rows[1], sgn, pairs[1][:, :, 1, :]),
+                ], lambda dst: nc.gpsimd.tensor_scalar(
+                    out=dst, in0=m[:], scalar1=mul, scalar2=add, op0=ALU.mult, op1=ALU.add
+                )
+            u = centre_early(early, v, g)
+            centre_late(u, late, v, g)
+            before, after, s = outer_taps(v, g)
             return u, [
                 lambda: add_tap(u[:, s : s + BANK], early[:], before),
                 lambda: add_tap(u[:, s + BANK : COLS], late[:, 0 : BANK - s], before),
                 lambda: add_tap(u[:, 0 : BANK - s], early[:, s:BANK], after),
                 lambda: add_tap(u[:, BANK - s : COLS - s], late[:], after),
-            ]
+            ], None
 
         def pool(u, pieces):
             pooled = pooled_pool.tile([P, OUT_COLS], F32, tag="pooled")
@@ -273,8 +323,25 @@ def tile_timeception_pa_t_e_kernel(tc, x, w_words, w_scales, b, dw, bn, out):
 
         for chunk in range(CHUNKS):
             load(CHUNKS + chunk)
-        for v in BRANCH_ORDER:
-            load_codes(v, 1)
+        load_codes(range(BRANCHES), 1)
+
+        begun = []
+        late_quantise = []
+        early_taps = []
+        for turn, v in enumerate(CONVOLUTIONS):
+            bank = multiply(0, v, 0, 0)
+            u = centre_early(bank, v, 0)
+            begun.append((u, bank))
+            for index in ((4, 5), (6, 7), ())[turn]:
+                late_quantise.append(head_flip(index))
+            before, after, s = outer_taps(v, 0)
+            early_taps.append(lambda u=u, bank=bank, s=s, tap=before: add_tap(u[:, s:BANK], bank[:, 0 : BANK - s], tap))
+            early_taps.append(lambda u=u, bank=bank, s=s, tap=after: add_tap(u[:, 0 : BANK - s], bank[:, s:BANK], tap))
+        for turn, tap in enumerate(early_taps):
+            tap()
+            if turn < len(late_quantise):
+                late_quantise[turn]()
+
         flips = [(part, kp, chunk) for part in range(1, SLICES) for kp in range(PASSES) for chunk in range(CHUNKS)]
         flipped_so_far = 0
         wide = None
@@ -290,20 +357,32 @@ def tile_timeception_pa_t_e_kernel(tc, x, w_words, w_scales, b, dw, bn, out):
         to_emit = []
         emitted = 0
 
-        def pool_last(pieces=1):
-            u, n, v, g = to_pool
-            pooled_tiles.setdefault((n, v), {})[g] = pool(u, pieces)
+        def note_pooled(pooled, n, v, g):
+            pooled_tiles.setdefault((n, v), {})[g] = pooled
             if len(pooled_tiles[(n, v)]) == GROUPS:
                 pooled_now.append((n, v))
 
-        ctx.enter_context(tc.manual_schedule(engines={mybir.EngineType.PE, mybir.EngineType.Activation, mybir.EngineType.DVE}))
-        for place, (n, v, g) in enumerate(units):
-            early = first_early if place == 0 else multiply(n, v, g, 0)
+        def pool_last(pieces=1):
+            u, n, v, g = to_pool
+            note_pooled(pool(u, pieces), n, v, g)
+
+        def start_unit(place):
+            n, v, g = units[place]
+            if place < len(begun):
+                u, early = begun[place]
+                return u, finish_convolution(u, early, multiply(n, v, g, 1), v, g), None
+            early = multiply(n, v, g, 0)
             late = multiply(n, v, g, 1)
-            u, steps = start_branch(early, late, v, g)
+            return start_branch(early, late, v, g)
+
+        started = []
+        for place, (n, v, g) in enumerate(units):
+            while len(started) < min(place + 1 + LEAD, len(units)):
+                started.append(start_unit(len(started)))
+            u, steps, finish = started[place]
             waiting = len([item for item in to_emit[emitted:] if item[0] <= place])
             emits = min(waiting, 1 if flipped_so_far < len(flips) else 2)
-            turns = 0 if place < FIRST_FLIP_UNIT else TURNS[v] - emits
+            turns = TURNS[v] - emits
             for part, kp, chunk in flips[flipped_so_far : flipped_so_far + turns]:
                 if kp == 0:
                     load((part + 1) * CHUNKS + chunk)
@@ -313,24 +392,28 @@ def tile_timeception_pa_t_e_kernel(tc, x, w_words, w_scales, b, dw, bn, out):
                 if chunk == CHUNKS - 1:
                     filled.append((part, kp, slice(0, COLS), wide[:]))
             flipped_so_far += turns
-            if v != 4:
-                for step in steps:
-                    step()
+            first_steps = len(steps) if finish is None else len(steps) // 2
+            for step in steps[:first_steps]:
+                step()
             if to_pool is not None:
                 pool_last()
-            room = {0: 2, 4: 1}.get(v, 0)
+            room = {0: 1, 4: 1}.get(v, 0)
             while quantised < len(to_quantise) and (
                 room > 0 or first_use[to_quantise[quantised][0]] - QUANTISE_AHEAD <= place
             ):
                 quantise(*to_quantise[quantised])
                 quantised += 1
                 room -= 1
-            if v == 4:
-                for step in steps:
-                    step()
+            for step in steps[first_steps:]:
+                step()
+            to_pool = (u, n, v, g)
+            if finish is not None:
+                pooled = pooled_pool.tile([P, OUT_COLS], F32, tag="pooled")
+                finish(pooled[:])
+                note_pooled(pooled, n, v, g)
+                to_pool = None
             to_quantise.extend(filled)
             filled.clear()
-            to_pool = (u, n, v, g)
             for turn in range(emits):
                 emit(*to_emit[emitted][1])
                 emitted += 1

@@ -69,6 +69,8 @@ def tile_timeception_pa_t_e_kernel(tc, x, w_words, w_scales, b, dw, bn, out):
 
         w_codes = const.tile([P, BRANCHES * GROUPS * PASSES, CB], U32, align_bytes=64)
         w_planes = const.tile([P, BRANCHES * GROUPS * PASSES, CB], U8, align_bytes=64)
+        warm = const.tile([P, 1], F32)
+        nc.vector.memset(warm[:], 1.0)
         nc.vector.memset(w_planes[:].bitcast(I32), 0)
         def load_planes(quad):
             nc.sync.dma_start(
@@ -77,33 +79,42 @@ def tile_timeception_pa_t_e_kernel(tc, x, w_words, w_scales, b, dw, bn, out):
             )
 
         w_words_by_pass = w_words.rearrange("(v gk) p o t -> gk p v (o t)", gk=GROUPS * PASSES).bitcast(I32)
+        w_words_by_branch = w_words.rearrange("(v g k) p o t -> (v g) p k (o t)", g=GROUPS, k=PASSES).bitcast(I32)
         w_codes_by_pass = w_codes[:].rearrange("p (v gk) o -> p gk v o", gk=GROUPS * PASSES)
 
         def load_codes(branches, g):
-            v = slice(branches[0], branches[-1] + 1)
+            v = branches[0]
+            if len(branches) == 1:
+                first = (v * GROUPS + g) * PASSES
+                nc.sync.dma_start(
+                    out=w_codes[:, first : first + PASSES, :].bitcast(I32), in_=w_words_by_branch[v * GROUPS + g]
+                )
+                return
             for gk in range(g * PASSES, (g + 1) * PASSES):
-                nc.sync.dma_start(out=w_codes_by_pass[:, gk, v, :].bitcast(I32), in_=w_words_by_pass[gk, :, v, :])
+                nc.sync.dma_start(
+                    out=w_codes_by_pass[:, gk, v : branches[-1] + 1, :].bitcast(I32),
+                    in_=w_words_by_pass[gk, :, v : branches[-1] + 1, :],
+                )
 
         n_b, n_dw, n_bn = BRANCHES * GROUPS, 3 * 3 * GROUPS, BRANCHES * 4 * GROUPS
         rows_bf = const.tile([P, CB], BF16)
         nc.gpsimd.memset(rows_bf[:], 0.0)
+        nc.gpsimd.dma_start(out=rows_bf[n_b + n_dw : n_b + n_dw + n_bn, :], in_=bn.rearrange("v j g o -> (v j g) o"))
+        ident = const.tile([P, P], F32)
+        make_identity(nc, ident[:])
         load(0)
         load(1)
-        nc.scalar.dma_start(out=rows_bf[n_b + n_dw : n_b + n_dw + n_bn, :], in_=bn.rearrange("v j g o -> (v j g) o"))
         nc.scalar.dma_start(out=rows_bf[n_b : n_b + n_dw, :], in_=dw.rearrange("i k g o -> (i k g) o"))
         nc.scalar.dma_start(out=rows_bf[0:n_b, :], in_=b.rearrange("v g o -> (v g) o"))
-        load_codes(CONVOLUTIONS, 0)
-        load(2)
+        load_codes(CONVOLUTIONS[:1], 0)
         for quad in range(4):
             load_planes(quad)
+        load(2)
+        load_codes(CONVOLUTIONS[1:], 0)
         load(3)
         for v in FIRST_ORDER[len(CONVOLUTIONS) :]:
             load_codes((v,), 0)
-        ident = const.tile([P, P], F32)
-        make_identity(nc, ident[:])
 
-        warm = const.tile([P, 1], F32)
-        nc.vector.memset(warm[:], 1.0)
         nc.scalar.activation(out=warm[:], in_=warm[:], func=ACT.Abs_reciprocal_sqrt)
 
         codes = {}
@@ -130,10 +141,10 @@ def tile_timeception_pa_t_e_kernel(tc, x, w_words, w_scales, b, dw, bn, out):
             x_codes, x_planes = codes[part]
             nc.vector.quantize_mx(out=x_codes[:, kp, cols].bitcast(FP8X4), scales=x_planes[:, kp, cols], in_=grouped)
 
-        def head_flip(index):
+        def head_flip(index, engine="scalar"):
             chunk, kp = index // PASSES, index % PASSES
             narrow = narrow_pool.tile([P, 4 * CHUNK], BF16, align_bytes=64, tag="narrow")
-            flip(0, kp, chunk, narrow[:], "scalar")
+            flip(0, kp, chunk, narrow[:], engine)
             return lambda: quantise(0, kp, slice(chunk * CHUNK, (chunk + 1) * CHUNK), narrow[:])
 
         def multiply(n, v, g, half):
@@ -156,7 +167,7 @@ def tile_timeception_pa_t_e_kernel(tc, x, w_words, w_scales, b, dw, bn, out):
         ctx.enter_context(tc.manual_schedule(engines={mybir.EngineType.PE, mybir.EngineType.Activation, mybir.EngineType.DVE}))
         ident_bf = const.tile([P, P], BF16)
         nc.vector.tensor_copy(out=ident_bf[:], in_=ident[:])
-        head_quantise = [head_flip(0), head_flip(1)]
+        head_quantise = [head_flip(0), head_flip(1, "vector")]
         turned = acc_psum.tile([P, BANK], F32, tag="acc")
         nc.tensor.matmul(turned[:, 0:P], lhsT=rows_bf[:], rhs=ident_bf[:], start=True, stop=True)
 
@@ -171,8 +182,6 @@ def tile_timeception_pa_t_e_kernel(tc, x, w_words, w_scales, b, dw, bn, out):
         bias, taps, (gamma, beta, mean, var) = views(turned)
         scale = const.tile([P, BRANCHES, GROUPS], F32)
         nc.scalar.activation(out=scale[:], in_=var, func=ACT.Abs_reciprocal_sqrt, bias=EPS)
-        params = const.tile([P, P], F32)
-        nc.scalar.copy(out=params[:], in_=turned[:, 0:P])
         head_quantise.append(head_flip(2))
         head_quantise.append(head_flip(3))
         conv_shape = [P, 3, 3, GROUPS]
@@ -184,18 +193,20 @@ def tile_timeception_pa_t_e_kernel(tc, x, w_words, w_scales, b, dw, bn, out):
         c_first = const.tile([P, 3, GROUPS], F32)
         c_last = const.tile([P, 3, GROUPS], F32)
         head_quantise[0]()
-        nc.vector.tensor_mul(out=scale[:], in0=scale[:], in1=gamma)
         head_quantise[1]()
+        nc.vector.tensor_mul(out=scale[:], in0=scale[:], in1=gamma)
         nc.vector.tensor_mul(out=s_taps[:], in0=scale[:, 1:4, :].unsqueeze(2).to_broadcast(conv_shape), in1=taps)
         nc.vector.tensor_mul(out=shift[:], in0=scale[:], in1=mean)
         nc.vector.tensor_mul(out=tap_bias[:], in0=s_taps[:], in1=bias[:, 1:4, :].unsqueeze(2).to_broadcast(conv_shape))
         nc.vector.tensor_sub(out=shift[:], in0=beta, in1=shift[:])
-        nc.vector.tensor_add(out=c_centre[:], in0=shift[:, 1:4, :], in1=tap_bias[:, :, 1, :])
         head_quantise[2]()
+        nc.vector.tensor_add(out=c_centre[:], in0=shift[:, 1:4, :], in1=tap_bias[:, :, 1, :])
+        head_quantise[3]()
         nc.vector.tensor_add(out=c_first[:], in0=c_centre[:], in1=tap_bias[:, :, 2, :])
         nc.vector.tensor_add(out=c_last[:], in0=c_centre[:], in1=tap_bias[:, :, 0, :])
-        head_quantise[3]()
         nc.vector.tensor_add(out=c_inner[:], in0=c_first[:], in1=tap_bias[:, :, 0, :])
+        params = const.tile([P, P], F32)
+        nc.vector.tensor_copy(out=params[:], in_=turned[:, 0:P])
         bias, taps, (gamma, beta, mean, var) = views(params)
         offset = const.tile([P, BRANCHES, GROUPS], F32)
         nc.gpsimd.tensor_mul(out=offset[:], in0=scale[:], in1=bias)
@@ -315,6 +326,19 @@ def tile_timeception_pa_t_e_kernel(tc, x, w_words, w_scales, b, dw, bn, out):
             channels = rows[:, v * GROUPS * CB : (v + 1) * GROUPS * CB]
             nc.sync.dma_start(out=channels.rearrange("(a p) c -> p a c", p=P), in_=out_tile[:])
 
+        def emit_piece(pooled_by_group, n, v, piece):
+            flipped = flip_psum.tile([P, GROUPS, P], F32, tag="flip")
+            for g in range(GROUPS):
+                nc.tensor.transpose(flipped[:, g, :], pooled_by_group[g][:, piece * P : (piece + 1) * P], ident[:])
+            out_tile = out_pool.tile([P, GROUPS * CB], F32, tag="piece")
+            shuffled = out_tile[:].rearrange("p (o g) -> p o g", g=GROUPS)
+            if piece % 2 == 0:
+                nc.scalar.activation(out=shuffled, in_=flipped[:].rearrange("p g o -> p o g"), func=ACT.Relu)
+            else:
+                nc.vector.tensor_scalar_max(out=shuffled, in0=flipped[:].rearrange("p g o -> p o g"), scalar1=0.0)
+            first = n * OUT_COLS + piece * P
+            nc.sync.dma_start(out=out_rows[first : first + P, v * GROUPS * CB : (v + 1) * GROUPS * CB], in_=out_tile[:])
+
         units = []
         for n in range(BATCH - 1):
             for g in range(GROUPS):
@@ -421,7 +445,8 @@ def tile_timeception_pa_t_e_kernel(tc, x, w_words, w_scales, b, dw, bn, out):
                 to_emit.extend([(place + 1 + EMIT_LAG, (pooled_tiles[key], key[0], key[1], pair)) for pair in range(2)])
             pooled_now.clear()
         pool_last(2)
-        for key in pooled_now:
-            to_emit.extend([(0, (pooled_tiles[key], key[0], key[1], pair)) for pair in range(2)])
         for item in to_emit[emitted:]:
             emit(*item[1])
+        for key in pooled_now:
+            for piece in range(OUT_COLS // P):
+                emit_piece(pooled_tiles[key], key[0], key[1], piece)

@@ -99,13 +99,23 @@ def tile_timeception_pa_t_e_kernel(tc, x, w_words, w_scales, b, dw, bn, out):
         n_b, n_dw, n_bn = BRANCHES * GROUPS, 3 * 3 * GROUPS, BRANCHES * 4 * GROUPS
         rows_bf = const.tile([P, CB], BF16)
         nc.gpsimd.memset(rows_bf[:], 0.0)
-        nc.gpsimd.dma_start(out=rows_bf[n_b + n_dw : n_b + n_dw + n_bn, :], in_=bn.rearrange("v j g o -> (v j g) o"))
         ident = const.tile([P, P], F32)
         make_identity(nc, ident[:])
+
+        def load_rows(first, source):
+            done = 0
+            while done < source.shape[0]:
+                count = 1
+                while 2 * count <= source.shape[0] - done:
+                    count *= 2
+                nc.sync.dma_start(out=rows_bf[first + done : first + done + count, :], in_=source[done : done + count, :])
+                done += count
+
         load(0)
+        load_rows(n_b + n_dw, bn.rearrange("v j g o -> (v j g) o"))
+        load_rows(n_b, dw.rearrange("i k g o -> (i k g) o"))
+        load_rows(0, b.rearrange("v g o -> (v g) o"))
         load(1)
-        nc.scalar.dma_start(out=rows_bf[n_b : n_b + n_dw, :], in_=dw.rearrange("i k g o -> (i k g) o"))
-        nc.scalar.dma_start(out=rows_bf[0:n_b, :], in_=b.rearrange("v g o -> (v g) o"))
         load_codes(CONVOLUTIONS[:1], 0)
         for quad in range(4):
             load_planes(quad)
@@ -167,7 +177,7 @@ def tile_timeception_pa_t_e_kernel(tc, x, w_words, w_scales, b, dw, bn, out):
         ctx.enter_context(tc.manual_schedule(engines={mybir.EngineType.PE, mybir.EngineType.Activation, mybir.EngineType.DVE}))
         ident_bf = const.tile([P, P], BF16)
         nc.vector.tensor_copy(out=ident_bf[:], in_=ident[:])
-        head_quantise = [head_flip(0), head_flip(1, "vector")]
+        head_quantise = [head_flip(0)]
         turned = acc_psum.tile([P, BANK], F32, tag="acc")
         nc.tensor.matmul(turned[:, 0:P], lhsT=rows_bf[:], rhs=ident_bf[:], start=True, stop=True)
 
@@ -182,6 +192,7 @@ def tile_timeception_pa_t_e_kernel(tc, x, w_words, w_scales, b, dw, bn, out):
         bias, taps, (gamma, beta, mean, var) = views(turned)
         scale = const.tile([P, BRANCHES, GROUPS], F32)
         nc.scalar.activation(out=scale[:], in_=var, func=ACT.Abs_reciprocal_sqrt, bias=EPS)
+        head_quantise.append(head_flip(1, "vector"))
         head_quantise.append(head_flip(2))
         head_quantise.append(head_flip(3))
         conv_shape = [P, 3, 3, GROUPS]
@@ -230,13 +241,11 @@ def tile_timeception_pa_t_e_kernel(tc, x, w_words, w_scales, b, dw, bn, out):
         def outer_taps(v, g):
             return s_taps[:, v - 1, 0, g : g + 1], s_taps[:, v - 1, 2, g : g + 1], v * PIXELS
 
-        def centre_early(early, v, g):
-            u = work.tile([P, COLS], F32, tag="u")
+        def centre_early(u, early, v, g):
             i, s = v - 1, v * PIXELS
             centre = s_taps[:, i, 1, g : g + 1]
             affine(u[:, 0:s], early[:, 0:s], centre, c_first[:, i, g : g + 1])
             affine(u[:, s:BANK], early[:, s:BANK], centre, c_inner[:, i, g : g + 1])
-            return u
 
         def centre_late(u, late, v, g):
             i, s = v - 1, v * PIXELS
@@ -244,56 +253,73 @@ def tile_timeception_pa_t_e_kernel(tc, x, w_words, w_scales, b, dw, bn, out):
             affine(u[:, BANK : COLS - s], late[:, 0 : BANK - s], centre, c_inner[:, i, g : g + 1])
             affine(u[:, COLS - s : COLS], late[:, BANK - s : BANK], centre, c_last[:, i, g : g + 1])
 
-        def finish_convolution(u, early, late, v, g):
-            centre_late(u, late, v, g)
-            before, after, s = outer_taps(v, g)
-            return [
-                lambda: add_tap(u[:, BANK : BANK + s], early[:, BANK - s : BANK], before),
-                lambda: add_tap(u[:, BANK + s : COLS], late[:, 0 : BANK - s], before),
-                lambda: add_tap(u[:, BANK - s : BANK], late[:, 0:s], after),
-                lambda: add_tap(u[:, BANK : COLS - s], late[:, s:BANK], after),
-            ]
+        def half_pairs(bank):
+            return bank[:].rearrange("p (t two q) -> p t two q", two=2, q=PIXELS)
 
-        def start_branch(early, late, v, g):
-            mul, add = scale[:, v, g : g + 1], offset[:, v, g : g + 1]
-            if v in (0, 4):
-                m = light_pool.tile([P, OUT_COLS], F32, tag="m")
-                pairs = [
-                    bank[:].rearrange("p (t two q) -> p t two q", two=2, q=PIXELS) for bank in (early, late)
-                ]
-                m_rows = m[:].rearrange("p (t q) -> p t q", q=PIXELS)
-                half_rows = [m_rows[:, 0 : TIME // 4, :], m_rows[:, TIME // 4 : TIME // 2, :]]
+        def light_branch(n, v, g):
+            mul, add, sgn = scale[:, v, g : g + 1], offset[:, v, g : g + 1], sign[:, v, g : g + 1]
+            m = light_pool.tile([P, OUT_COLS], F32, tag="m")
+            m_rows = m[:].rearrange("p (t q) -> p t q", q=PIXELS)
+            quarter = TIME // 4
+            half_rows = [m_rows[:, 0:quarter, :], m_rows[:, quarter : 2 * quarter, :]]
+            pairs = []
+
+            def products(half):
+                bank = multiply(n, v, g, half)
+                pairs.append(half_pairs(bank))
+                if v == 0:
+                    scaled_copy(half_rows[half], pairs[half][:, :, 1, :], mul)
+                elif half == 0:
+                    scaled_copy(m_rows[:, 0 : quarter - 1, :], pairs[0][:, 1:, 0, :], sgn)
+                else:
+                    scaled_copy(m_rows[:, quarter - 1 : 2 * quarter - 1, :], pairs[1][:, :, 0, :], sgn)
+                    scaled_copy(m[:, OUT_COLS - PIXELS : OUT_COLS], bank[:, BANK - PIXELS : BANK], sgn)
+
+            def affine_of(factor):
+                return lambda dst: nc.gpsimd.tensor_scalar(
+                    out=dst, in0=m[:], scalar1=factor, scalar2=add, op0=ALU.mult, op1=ALU.add
+                )
+
             if v == 0:
-                for rows, pair in zip(half_rows, pairs):
-                    scaled_copy(rows, pair[:, :, 1, :], mul)
-                return m, [
+                return products, m, [
                     lambda: sttmax(half_rows[0], pairs[0][:, :, 0, :], mul, half_rows[0]),
                     lambda: sttmax(half_rows[1], pairs[1][:, :, 0, :], mul, half_rows[1]),
-                ], lambda dst: nc.gpsimd.tensor_scalar(
-                    out=dst, in0=m[:], scalar1=1.0, scalar2=add, op0=ALU.mult, op1=ALU.add
-                )
-            if v == 4:
-                sgn = sign[:, v, g : g + 1]
-                s = PIXELS
-                scaled_copy(m_rows[:, 0 : TIME // 4 - 1, :], pairs[0][:, 1:, 0, :], sgn)
-                scaled_copy(m_rows[:, TIME // 4 - 1 : TIME // 2 - 1, :], pairs[1][:, :, 0, :], sgn)
-                scaled_copy(m[:, OUT_COLS - s : OUT_COLS], late[:, BANK - s : BANK], sgn)
-                return m, [
-                    lambda: sttmax(half_rows[0], pairs[0][:, :, 0, :], sgn, half_rows[0]),
-                    lambda: sttmax(half_rows[1], pairs[1][:, :, 0, :], sgn, half_rows[1]),
-                    lambda: sttmax(half_rows[0], half_rows[0], sgn, pairs[0][:, :, 1, :]),
-                    lambda: sttmax(half_rows[1], half_rows[1], sgn, pairs[1][:, :, 1, :]),
-                ], lambda dst: nc.gpsimd.tensor_scalar(
-                    out=dst, in0=m[:], scalar1=mul, scalar2=add, op0=ALU.mult, op1=ALU.add
-                )
-            u = centre_early(early, v, g)
-            centre_late(u, late, v, g)
+                ], affine_of(1.0)
+            return products, m, [
+                lambda: sttmax(half_rows[0], pairs[0][:, :, 0, :], sgn, half_rows[0]),
+                lambda: sttmax(half_rows[1], pairs[1][:, :, 0, :], sgn, half_rows[1]),
+                lambda: sttmax(half_rows[0], half_rows[0], sgn, pairs[0][:, :, 1, :]),
+                lambda: sttmax(half_rows[1], half_rows[1], sgn, pairs[1][:, :, 1, :]),
+            ], affine_of(mul)
+
+        def convolution(n, v, g, u=None, early=None):
             before, after, s = outer_taps(v, g)
-            return u, [
-                lambda: add_tap(u[:, s : s + BANK], early[:], before),
-                lambda: add_tap(u[:, s + BANK : COLS], late[:, 0 : BANK - s], before),
-                lambda: add_tap(u[:, 0 : BANK - s], early[:, s:BANK], after),
-                lambda: add_tap(u[:, BANK - s : COLS - s], late[:], after),
+            begun = u is not None
+            if not begun:
+                u = work.tile([P, COLS], F32, tag="u")
+            banks = [early]
+
+            def products(half):
+                if half == 0:
+                    if not begun:
+                        banks[0] = multiply(n, v, g, 0)
+                        centre_early(u, banks[0], v, g)
+                else:
+                    banks.append(multiply(n, v, g, 1))
+                    centre_late(u, banks[1], v, g)
+
+            if begun:
+                return products, u, [
+                    lambda: add_tap(u[:, BANK : BANK + s], banks[0][:, BANK - s : BANK], before),
+                    lambda: add_tap(u[:, BANK + s : COLS], banks[1][:, 0 : BANK - s], before),
+                    lambda: add_tap(u[:, BANK - s : BANK], banks[1][:, 0:s], after),
+                    lambda: add_tap(u[:, BANK : COLS - s], banks[1][:, s:BANK], after),
+                ], None
+            return products, u, [
+                lambda: add_tap(u[:, s : s + BANK], banks[0][:], before),
+                lambda: add_tap(u[:, s + BANK : COLS], banks[1][:, 0 : BANK - s], before),
+                lambda: add_tap(u[:, 0 : BANK - s], banks[0][:, s:BANK], after),
+                lambda: add_tap(u[:, BANK - s : COLS - s], banks[1][:], after),
             ], None
 
         def pool(u, pieces):
@@ -354,7 +380,8 @@ def tile_timeception_pa_t_e_kernel(tc, x, w_words, w_scales, b, dw, bn, out):
         early_taps = []
         for turn, v in enumerate(CONVOLUTIONS):
             bank = multiply(0, v, 0, 0)
-            u = centre_early(bank, v, 0)
+            u = work.tile([P, COLS], F32, tag="u")
+            centre_early(u, bank, v, 0)
             begun.append((u, bank))
             for index in ((4, 5), (6, 7), ())[turn]:
                 late_quantise.append(head_flip(index))
@@ -390,32 +417,38 @@ def tile_timeception_pa_t_e_kernel(tc, x, w_words, w_scales, b, dw, bn, out):
             u, n, v, g = to_pool
             note_pooled(pool(u, pieces), n, v, g)
 
-        def start_unit(place):
-            n, v, g = units[place]
-            if place < len(begun):
-                u, early = begun[place]
-                return u, finish_convolution(u, early, multiply(n, v, g, 1), v, g), None
-            early = multiply(n, v, g, 0)
-            late = multiply(n, v, g, 1)
-            return start_branch(early, late, v, g)
-
         started = []
         for place, (n, v, g) in enumerate(units):
+            products = []
             while len(started) < min(place + 1 + LEAD, len(units)):
-                started.append(start_unit(len(started)))
-            u, steps, finish = started[place]
+                unit = units[len(started)]
+                if len(started) < len(begun):
+                    started.append(convolution(*unit, *begun[len(started)]))
+                else:
+                    started.append((light_branch if unit[1] in (0, 4) else convolution)(*unit))
+                products.extend([(started[-1][0], 0), (started[-1][0], 1)])
+            u, steps, finish = started[place][1:]
             waiting = len([item for item in to_emit[emitted:] if item[0] <= place])
             emits = min(waiting, 1 if flipped_so_far < len(flips) else 2)
             turns = TURNS[v] - emits
-            for part, kp, chunk in flips[flipped_so_far : flipped_so_far + turns]:
-                if kp == 0:
-                    load((part + 1) * CHUNKS + chunk)
-                if chunk == 0:
-                    wide = wide_pool.tile([P, 4 * COLS], BF16, align_bytes=64, tag="wide")
-                flip(part, kp, chunk, wide[:, 4 * CHUNK * chunk : 4 * CHUNK * (chunk + 1)], "scalar")
-                if chunk == CHUNKS - 1:
-                    filled.append((part, kp, slice(0, COLS), wide[:]))
+            banks = [("flip", item) for item in flips[flipped_so_far : flipped_so_far + turns]]
             flipped_so_far += turns
+            banks.extend([("emit", item[1]) for item in to_emit[emitted : emitted + emits]])
+            emitted += emits
+            for product, half in products:
+                product(half)
+            for kind, item in banks:
+                if kind == "emit":
+                    emit(*item)
+                else:
+                    part, kp, chunk = item
+                    if kp == 0:
+                        load((part + 1) * CHUNKS + chunk)
+                    if chunk == 0:
+                        wide = wide_pool.tile([P, 4 * COLS], BF16, align_bytes=64, tag="wide")
+                    flip(part, kp, chunk, wide[:, 4 * CHUNK * chunk : 4 * CHUNK * (chunk + 1)], "scalar")
+                    if chunk == CHUNKS - 1:
+                        filled.append((part, kp, slice(0, COLS), wide[:]))
             first_steps = len(steps) if finish is None else len(steps) // 2
             for step in steps[:first_steps]:
                 step()
@@ -438,9 +471,6 @@ def tile_timeception_pa_t_e_kernel(tc, x, w_words, w_scales, b, dw, bn, out):
                 to_pool = None
             to_quantise.extend(filled)
             filled.clear()
-            for turn in range(emits):
-                emit(*to_emit[emitted][1])
-                emitted += 1
             for key in pooled_now:
                 to_emit.extend([(place + 1 + EMIT_LAG, (pooled_tiles[key], key[0], key[1], pair)) for pair in range(2)])
             pooled_now.clear()

@@ -28,7 +28,7 @@ LOADS = SLICES * CHUNKS
 BRANCH_ORDER = (1, 0, 2, 4, 3)
 CONVOLUTIONS = (1, 2, 3)
 FIRST_ORDER = CONVOLUTIONS + (0, 4)
-LAST_UNITS = ((4, 0), (1, 0), (4, 1), (1, 1), (0, 0), (2, 0), (0, 1), (2, 1), (3, 0), (3, 1))
+LAST_UNITS = ((4, 0), (1, 0), (2, 0), (4, 1), (1, 1), (0, 0), (2, 1), (0, 1), (3, 0), (3, 1))
 TURNS = {0: 2, 1: 3, 2: 3, 3: 3, 4: 2}
 LEAD = 1
 QUANTISE_AHEAD = 4
@@ -222,6 +222,8 @@ def tile_timeception_pa_t_e_kernel(tc, x, w_words, w_scales, b, dw, bn, out):
         offset = const.tile([P, BRANCHES, GROUPS], F32)
         nc.gpsimd.tensor_mul(out=offset[:], in0=scale[:], in1=bias)
         nc.gpsimd.tensor_add(out=offset[:], in0=offset[:], in1=shift[:])
+        minus_tap_bias = const.tile(conv_shape, F32)
+        nc.gpsimd.tensor_scalar(out=minus_tap_bias[:], in0=tap_bias[:], scalar1=-1.0, scalar2=0.0, op0=ALU.mult, op1=ALU.add)
         sign = const.tile([P, BRANCHES, GROUPS], F32)
         nc.gpsimd.tensor_scalar(out=sign[:], in0=gamma, scalar1=0.0, scalar2=2.0, op0=ALU.is_ge, op1=ALU.mult)
         nc.gpsimd.tensor_scalar(out=sign[:], in0=sign[:], scalar1=1.0, scalar2=-1.0, op0=ALU.mult, op1=ALU.add)
@@ -241,17 +243,28 @@ def tile_timeception_pa_t_e_kernel(tc, x, w_words, w_scales, b, dw, bn, out):
         def outer_taps(v, g):
             return s_taps[:, v - 1, 0, g : g + 1], s_taps[:, v - 1, 2, g : g + 1], v * PIXELS
 
-        def centre_early(u, early, v, g):
+        def centre_early(u, early, v, g, whole=False):
             i, s = v - 1, v * PIXELS
             centre = s_taps[:, i, 1, g : g + 1]
+            if whole:
+                affine(u[:, 0:BANK], early[:], centre, c_inner[:, i, g : g + 1])
+                return
             affine(u[:, 0:s], early[:, 0:s], centre, c_first[:, i, g : g + 1])
             affine(u[:, s:BANK], early[:, s:BANK], centre, c_inner[:, i, g : g + 1])
 
-        def centre_late(u, late, v, g):
+        def centre_late(u, late, v, g, whole=False):
             i, s = v - 1, v * PIXELS
             centre = s_taps[:, i, 1, g : g + 1]
+            if whole:
+                affine(u[:, BANK:COLS], late[:], centre, c_inner[:, i, g : g + 1])
+                return
             affine(u[:, BANK : COLS - s], late[:, 0 : BANK - s], centre, c_inner[:, i, g : g + 1])
             affine(u[:, COLS - s : COLS], late[:, BANK - s : BANK], centre, c_last[:, i, g : g + 1])
+
+        def outside(dst, v, tap, g):
+            nc.gpsimd.tensor_scalar(
+                out=dst, in0=dst, scalar1=1.0, scalar2=minus_tap_bias[:, v - 1, tap, g : g + 1], op0=ALU.mult, op1=ALU.add
+            )
 
         def half_pairs(bank):
             return bank[:].rearrange("p (t two q) -> p t two q", two=2, q=PIXELS)
@@ -303,10 +316,10 @@ def tile_timeception_pa_t_e_kernel(tc, x, w_words, w_scales, b, dw, bn, out):
                 if half == 0:
                     if not begun:
                         banks[0] = multiply(n, v, g, 0)
-                        centre_early(u, banks[0], v, g)
+                        centre_early(u, banks[0], v, g, True)
                 else:
                     banks.append(multiply(n, v, g, 1))
-                    centre_late(u, banks[1], v, g)
+                    centre_late(u, banks[1], v, g, not begun)
 
             if begun:
                 return products, u, [
@@ -320,6 +333,8 @@ def tile_timeception_pa_t_e_kernel(tc, x, w_words, w_scales, b, dw, bn, out):
                 lambda: add_tap(u[:, s + BANK : COLS], banks[1][:, 0 : BANK - s], before),
                 lambda: add_tap(u[:, 0 : BANK - s], banks[0][:, s:BANK], after),
                 lambda: add_tap(u[:, BANK - s : COLS - s], banks[1][:], after),
+                lambda: outside(u[:, COLS - s : COLS], v, 2, g),
+                lambda: outside(u[:, 0:s], v, 0, g),
             ], None
 
         def pool(u, pieces):

@@ -305,7 +305,7 @@ def tile_timeception_pa_t_e_kernel(tc, x, w_words, w_scales, b, dw, bn, out):
                 lambda: sttmax(half_rows[1], half_rows[1], sgn, pairs[1][:, :, 1, :]),
             ], affine_of(mul)
 
-        def convolution(n, v, g, u=None, early=None):
+        def convolution(n, v, g, u=None, early=None, last=False):
             before, after, s = outer_taps(v, g)
             begun = u is not None
             if not begun:
@@ -316,10 +316,10 @@ def tile_timeception_pa_t_e_kernel(tc, x, w_words, w_scales, b, dw, bn, out):
                 if half == 0:
                     if not begun:
                         banks[0] = multiply(n, v, g, 0)
-                        centre_early(u, banks[0], v, g, True)
+                        centre_early(u, banks[0], v, g, not last)
                 else:
                     banks.append(multiply(n, v, g, 1))
-                    centre_late(u, banks[1], v, g, not begun)
+                    centre_late(u, banks[1], v, g, not begun and not last)
 
             if begun:
                 return products, u, [
@@ -328,14 +328,13 @@ def tile_timeception_pa_t_e_kernel(tc, x, w_words, w_scales, b, dw, bn, out):
                     lambda: add_tap(u[:, BANK - s : BANK], banks[1][:, 0:s], after),
                     lambda: add_tap(u[:, BANK : COLS - s], banks[1][:, s:BANK], after),
                 ], None
+            ends = [] if last else [lambda: outside(u[:, COLS - s : COLS], v, 2, g), lambda: outside(u[:, 0:s], v, 0, g)]
             return products, u, [
                 lambda: add_tap(u[:, s : s + BANK], banks[0][:], before),
                 lambda: add_tap(u[:, s + BANK : COLS], banks[1][:, 0 : BANK - s], before),
                 lambda: add_tap(u[:, 0 : BANK - s], banks[0][:, s:BANK], after),
                 lambda: add_tap(u[:, BANK - s : COLS - s], banks[1][:], after),
-                lambda: outside(u[:, COLS - s : COLS], v, 2, g),
-                lambda: outside(u[:, 0:s], v, 0, g),
-            ], None
+            ] + ends, None
 
         def pool(u, pieces):
             pooled = pooled_pool.tile([P, OUT_COLS], F32, tag="pooled")
@@ -367,10 +366,10 @@ def tile_timeception_pa_t_e_kernel(tc, x, w_words, w_scales, b, dw, bn, out):
             channels = rows[:, v * GROUPS * CB : (v + 1) * GROUPS * CB]
             nc.sync.dma_start(out=channels.rearrange("(a p) c -> p a c", p=P), in_=out_tile[:])
 
-        def emit_piece(pooled_by_group, n, v, piece):
-            flipped = flip_psum.tile([P, GROUPS, P], F32, tag="flip")
-            for g in range(GROUPS):
-                nc.tensor.transpose(flipped[:, g, :], pooled_by_group[g][:, piece * P : (piece + 1) * P], ident[:])
+        def turn_piece(flipped, g, pooled, piece):
+            nc.tensor.transpose(flipped[:, g, :], pooled[:, piece * P : (piece + 1) * P], ident[:])
+
+        def store_piece(flipped, n, v, piece):
             out_tile = out_pool.tile([P, GROUPS * CB], F32, tag="piece")
             shuffled = out_tile[:].rearrange("p (o g) -> p o g", g=GROUPS)
             if piece % 2 == 0:
@@ -440,7 +439,10 @@ def tile_timeception_pa_t_e_kernel(tc, x, w_words, w_scales, b, dw, bn, out):
                 if len(started) < len(begun):
                     started.append(convolution(*unit, *begun[len(started)]))
                 else:
-                    started.append((light_branch if unit[1] in (0, 4) else convolution)(*unit))
+                    if unit[1] in (0, 4):
+                        started.append(light_branch(*unit))
+                    else:
+                        started.append(convolution(*unit, last=len(started) == len(units) - 1))
                 products.extend([(started[-1][0], 0), (started[-1][0], 1)])
             u, steps, finish = started[place][1:]
             waiting = len([item for item in to_emit[emitted:] if item[0] <= place])
@@ -464,7 +466,7 @@ def tile_timeception_pa_t_e_kernel(tc, x, w_words, w_scales, b, dw, bn, out):
                     flip(part, kp, chunk, wide[:, 4 * CHUNK * chunk : 4 * CHUNK * (chunk + 1)], "scalar")
                     if chunk == CHUNKS - 1:
                         filled.append((part, kp, slice(0, COLS), wide[:]))
-            first_steps = len(steps) if finish is None else len(steps) // 2
+            first_steps = len(steps) if finish is None and place < len(units) - 1 else len(steps) // 2
             for step in steps[:first_steps]:
                 step()
             if to_pool is not None:
@@ -489,9 +491,15 @@ def tile_timeception_pa_t_e_kernel(tc, x, w_words, w_scales, b, dw, bn, out):
             for key in pooled_now:
                 to_emit.extend([(place + 1 + EMIT_LAG, (pooled_tiles[key], key[0], key[1], pair)) for pair in range(2)])
             pooled_now.clear()
-        pool_last(2)
         for item in to_emit[emitted:]:
             emit(*item[1])
-        for key in pooled_now:
-            for piece in range(OUT_COLS // P):
-                emit_piece(pooled_tiles[key], key[0], key[1], piece)
+        u, n, v, g = to_pool
+        pieces = []
+        for piece in range(OUT_COLS // P):
+            flipped = acc_psum.tile([P, GROUPS, P], F32, tag="acc")
+            turn_piece(flipped, 1 - g, pooled_tiles[(n, v)][1 - g], piece)
+            pieces.append(flipped)
+        pooled = pool(u, len(pieces))
+        for piece, flipped in enumerate(pieces):
+            turn_piece(flipped, g, pooled, piece)
+            store_piece(flipped, n, v, piece)

from contextlib import ExitStack

import concourse.mybir as mybir
from concourse.masks import make_identity

F32 = mybir.dt.float32
BF16 = mybir.dt.bfloat16
I32 = mybir.dt.int32
U32 = mybir.dt.uint32
U8 = mybir.dt.uint8
FP8X4 = mybir.dt.float8_e4m3fn_x4
ALU = mybir.AluOpType
ACT = mybir.ActivationFunctionType

P = 128
BATCH, TIME, PIXELS = 4, 64, 16
GROUPS, K, CB, BRANCHES = 2, 1024, 128, 5
EPS = 1e-3
K_PASS = 4 * P
PASSES = K // K_PASS
COLS = TIME * PIXELS
BANK = 512
CHUNK = 2 * P
CHUNKS = COLS // CHUNK
OUT_COLS = COLS // 2
SLICES = BATCH * GROUPS
LOADS = SLICES * CHUNKS
BRANCH_ORDER = (1, 0, 2, 4, 3)
CONVOLUTIONS = (1, 2, 3)
FIRST_ORDER = CONVOLUTIONS + (0, 4)
LAST_UNITS = ((4, 0), (1, 0), (2, 0), (4, 1), (1, 1), (0, 0), (2, 1), (0, 1), (3, 0), (3, 1))
TURNS = {0: 2, 1: 3, 2: 3, 3: 3, 4: 2}
LEAD = 1
QUANTISE_AHEAD = 4
EMIT_LAG = 2

FLOPS = 2 * BATCH * COLS * GROUPS * K * BRANCHES * CB


def tile_timeception_pa_t_e_kernel(tc, x, w_words, w_scales, b, dw, bn, out):
    nc = tc.nc
    x_rows = x.rearrange("n t h w c -> (n t h w) c")
    out_rows = out.rearrange("n t h w c -> (n t h w) c")

    with ExitStack() as ctx:
        const = ctx.enter_context(tc.tile_pool(name="const", bufs=1))
        x_pool = ctx.enter_context(tc.tile_pool(name="x", bufs=2 * CHUNKS + 1))
        narrow_pool = ctx.enter_context(tc.tile_pool(name="narrow", bufs=4))
        wide_pool = ctx.enter_context(tc.tile_pool(name="wide", bufs=4))
        codes_pool = ctx.enter_context(tc.tile_pool(name="codes", bufs=5))
        work = ctx.enter_context(tc.tile_pool(name="work", bufs=5))
        light_pool = ctx.enter_context(tc.tile_pool(name="light", bufs=3))
        pooled_pool = ctx.enter_context(tc.tile_pool(name="pooled", bufs=20))
        out_pool = ctx.enter_context(tc.tile_pool(name="outp", bufs=6))
        flip_psum = ctx.enter_context(tc.psum_pool(name="flip", bufs=3))
        acc_psum = ctx.enter_context(tc.psum_pool(name="acc", bufs=5))

        x_tiles = {}

        def load(index):
            if index >= LOADS:
                return
            n, g, chunk = index // (GROUPS * CHUNKS), (index // CHUNKS) % GROUPS, index % CHUNKS
            x_tile = x_pool.tile([P, 2, K], BF16, tag="x")
            first = (n * CHUNKS + chunk) * CHUNK
            rows = x_rows[first : first + CHUNK, g * K : (g + 1) * K]
            nc.sync.dma_start(out=x_tile[:], in_=rows.rearrange("(a p) c -> p a c", p=P))
            x_tiles[index] = x_tile

        w_codes = const.tile([P, BRANCHES * GROUPS * PASSES, CB], U32, align_bytes=64)
        w_planes = const.tile([P, BRANCHES * GROUPS * PASSES, CB], U8, align_bytes=64)
        warm = const.tile([P, 1], F32)
        nc.vector.memset(warm[:], 1.0)
        nc.vector.memset(w_planes[:].bitcast(I32), 0)
        def load_planes(quad):
            nc.sync.dma_start(
                out=w_planes[32 * quad : 32 * quad + 4].bitcast(I32),
                in_=w_scales[:, 4 * quad : 4 * quad + 4, :].bitcast(I32).rearrange("e r o -> r e o"),
            )

        w_words_by_pass = w_words.rearrange("(v gk) p o t -> gk p v (o t)", gk=GROUPS * PASSES).bitcast(I32)
        w_words_by_branch = w_words.rearrange("(v g k) p o t -> (v g) p k (o t)", g=GROUPS, k=PASSES).bitcast(I32)
        w_codes_by_pass = w_codes[:].rearrange("p (v gk) o -> p gk v o", gk=GROUPS * PASSES)

        def load_codes(branches, g):
            v = branches[0]
            if len(branches) == 1:
                first = (v * GROUPS + g) * PASSES
                nc.sync.dma_start(
                    out=w_codes[:, first : first + PASSES, :].bitcast(I32), in_=w_words_by_branch[v * GROUPS + g]
                )
                return
            for gk in range(g * PASSES, (g + 1) * PASSES):
                nc.sync.dma_start(
                    out=w_codes_by_pass[:, gk, v : branches[-1] + 1, :].bitcast(I32),
                    in_=w_words_by_pass[gk, :, v : branches[-1] + 1, :],
                )

        n_b, n_dw, n_bn = BRANCHES * GROUPS, 3 * 3 * GROUPS, BRANCHES * 4 * GROUPS
        rows_bf = const.tile([P, CB], BF16)
        nc.gpsimd.memset(rows_bf[:], 0.0)
        ident = const.tile([P, P], F32)
        make_identity(nc, ident[:])

        def load_rows(first, source):
            done = 0
            while done < source.shape[0]:
                count = 1
                while 2 * count <= source.shape[0] - done:
                    count *= 2
                nc.sync.dma_start(out=rows_bf[first + done : first + done + count, :], in_=source[done : done + count, :])
                done += count

        load(0)
        load_rows(n_b + n_dw, bn.rearrange("v j g o -> (v j g) o"))
        load_rows(n_b, dw.rearrange("i k g o -> (i k g) o"))
        load_rows(0, b.rearrange("v g o -> (v g) o"))
        load(1)
        load_codes(CONVOLUTIONS[:1], 0)
        for quad in range(4):
            load_planes(quad)
        load(2)
        load_codes(CONVOLUTIONS[1:], 0)
        load(3)
        for v in FIRST_ORDER[len(CONVOLUTIONS) :]:
            load_codes((v,), 0)

        nc.scalar.activation(out=warm[:], in_=warm[:], func=ACT.Abs_reciprocal_sqrt)

        codes = {}

        def flip(part, kp, chunk, grouped, engine):
            x_tile = x_tiles[part * CHUNKS + chunk]
            if part not in codes:
                x_codes = codes_pool.tile([P, PASSES, COLS], U32, align_bytes=64, tag="codes")
                x_planes = codes_pool.tile([P, PASSES, COLS], U8, align_bytes=64, tag="planes")
                codes[part] = (x_codes, x_planes)
            flipped = flip_psum.tile([P, 2, 2, P], F32, tag="flip")
            for a in range(2):
                words = x_tile[:, a, :].bitcast(F32)
                for u in range(2):
                    nc.tensor.transpose(flipped[:, a, u, :], words[:, 256 * kp + u : 256 * (kp + 1) : 2], ident[:])
            dst = grouped.bitcast(F32).rearrange("p (a r u) -> p a r u", a=2, u=2)
            src = flipped[:].rearrange("p a u r -> p a r u")
            if engine == "scalar":
                nc.scalar.copy(out=dst, in_=src)
            else:
                nc.vector.tensor_copy(out=dst, in_=src)

        def quantise(part, kp, cols, grouped):
            x_codes, x_planes = codes[part]
            nc.vector.quantize_mx(out=x_codes[:, kp, cols].bitcast(FP8X4), scales=x_planes[:, kp, cols], in_=grouped)

        def head_flip(index, engine="scalar"):
            chunk, kp = index // PASSES, index % PASSES
            narrow = narrow_pool.tile([P, 4 * CHUNK], BF16, align_bytes=64, tag="narrow")
            flip(0, kp, chunk, narrow[:], engine)
            return lambda: quantise(0, kp, slice(chunk * CHUNK, (chunk + 1) * CHUNK), narrow[:])

        def multiply(n, v, g, half):
            x_codes, x_planes = codes[n * GROUPS + g]
            acc = acc_psum.tile([P, BANK], F32, tag="acc")
            cols = slice(half * BANK, (half + 1) * BANK)
            for kp in range(PASSES):
                e = (v * GROUPS + g) * PASSES + kp
                nc.tensor.matmul_mx(
                    out=acc[:],
                    lhsT=w_codes[:, e, :].bitcast(FP8X4),
                    lhsT_scale=w_planes[:, e, :],
                    rhs=x_codes[:, kp, cols].bitcast(FP8X4),
                    rhs_scale=x_planes[:, kp, cols],
                    start=(kp == 0),
                    stop=(kp == PASSES - 1),
                )
            return acc

        ctx.enter_context(tc.manual_schedule(engines={mybir.EngineType.PE, mybir.EngineType.Activation, mybir.EngineType.DVE}))
        ident_bf = const.tile([P, P], BF16)
        nc.vector.tensor_copy(out=ident_bf[:], in_=ident[:])
        head_quantise = [head_flip(0)]
        turned = acc_psum.tile([P, BANK], F32, tag="acc")
        nc.tensor.matmul(turned[:, 0:P], lhsT=rows_bf[:], rhs=ident_bf[:], start=True, stop=True)

        def views(columns):
            bn_columns = columns[:, n_b + n_dw : n_b + n_dw + n_bn].rearrange("p (v j g) -> p v j g", j=4, g=GROUPS)
            return (
                columns[:, 0:n_b].rearrange("p (v g) -> p v g", g=GROUPS),
                columns[:, n_b : n_b + n_dw].rearrange("p (i k g) -> p i k g", k=3, g=GROUPS),
                [bn_columns[:, :, j, :] for j in range(4)],
            )

        bias, taps, (gamma, beta, mean, var) = views(turned)
        scale = const.tile([P, BRANCHES, GROUPS], F32)
        nc.scalar.activation(out=scale[:], in_=var, func=ACT.Abs_reciprocal_sqrt, bias=EPS)
        head_quantise.append(head_flip(1, "vector"))
        head_quantise.append(head_flip(2))
        head_quantise.append(head_flip(3))
        conv_shape = [P, 3, 3, GROUPS]
        shift = const.tile([P, BRANCHES, GROUPS], F32)
        s_taps = const.tile(conv_shape, F32)
        tap_bias = const.tile(conv_shape, F32)
        c_centre = const.tile([P, 3, GROUPS], F32)
        c_inner = const.tile([P, 3, GROUPS], F32)
        c_first = const.tile([P, 3, GROUPS], F32)
        c_last = const.tile([P, 3, GROUPS], F32)
        head_quantise[0]()
        head_quantise[1]()
        nc.vector.tensor_mul(out=scale[:], in0=scale[:], in1=gamma)
        nc.vector.tensor_mul(out=s_taps[:], in0=scale[:, 1:4, :].unsqueeze(2).to_broadcast(conv_shape), in1=taps)
        nc.vector.tensor_mul(out=shift[:], in0=scale[:], in1=mean)
        nc.vector.tensor_mul(out=tap_bias[:], in0=s_taps[:], in1=bias[:, 1:4, :].unsqueeze(2).to_broadcast(conv_shape))
        nc.vector.tensor_sub(out=shift[:], in0=beta, in1=shift[:])
        head_quantise[2]()
        nc.vector.tensor_add(out=c_centre[:], in0=shift[:, 1:4, :], in1=tap_bias[:, :, 1, :])
        head_quantise[3]()
        nc.vector.tensor_add(out=c_first[:], in0=c_centre[:], in1=tap_bias[:, :, 2, :])
        nc.vector.tensor_add(out=c_last[:], in0=c_centre[:], in1=tap_bias[:, :, 0, :])
        nc.vector.tensor_add(out=c_inner[:], in0=c_first[:], in1=tap_bias[:, :, 0, :])
        params = const.tile([P, P], F32)
        nc.vector.tensor_copy(out=params[:], in_=turned[:, 0:P])
        bias, taps, (gamma, beta, mean, var) = views(params)
        offset = const.tile([P, BRANCHES, GROUPS], F32)
        nc.gpsimd.tensor_mul(out=offset[:], in0=scale[:], in1=bias)
        nc.gpsimd.tensor_add(out=offset[:], in0=offset[:], in1=shift[:])
        minus_tap_bias = const.tile(conv_shape, F32)
        nc.gpsimd.tensor_scalar(out=minus_tap_bias[:], in0=tap_bias[:], scalar1=-1.0, scalar2=0.0, op0=ALU.mult, op1=ALU.add)
        sign = const.tile([P, BRANCHES, GROUPS], F32)
        nc.gpsimd.tensor_scalar(out=sign[:], in0=gamma, scalar1=0.0, scalar2=2.0, op0=ALU.is_ge, op1=ALU.mult)
        nc.gpsimd.tensor_scalar(out=sign[:], in0=sign[:], scalar1=1.0, scalar2=-1.0, op0=ALU.mult, op1=ALU.add)

        def affine(dst, src, mul, add):
            nc.scalar.activation(out=dst, in_=src, func=ACT.Identity, scale=mul, bias=add)

        def scaled_copy(dst, src, mul):
            nc.scalar.activation(out=dst, in_=src, func=ACT.Copy, scale=mul)

        def sttmax(dst, src, mul, other):
            nc.vector.scalar_tensor_tensor(out=dst, in0=src, scalar=mul, in1=other, op0=ALU.mult, op1=ALU.max)

        def add_tap(dst, src, tap):
            nc.vector.scalar_tensor_tensor(out=dst, in0=src, scalar=tap, in1=dst, op0=ALU.mult, op1=ALU.add)

        def outer_taps(v, g):
            return s_taps[:, v - 1, 0, g : g + 1], s_taps[:, v - 1, 2, g : g + 1], v * PIXELS

        def centre_early(u, early, v, g, whole=False):
            i, s = v - 1, v * PIXELS
            centre = s_taps[:, i, 1, g : g + 1]
            if whole:
                affine(u[:, 0:BANK], early[:], centre, c_inner[:, i, g : g + 1])
                return
            affine(u[:, 0:s], early[:, 0:s], centre, c_first[:, i, g : g + 1])
            affine(u[:, s:BANK], early[:, s:BANK], centre, c_inner[:, i, g : g + 1])

        def centre_late(u, late, v, g, whole=False):
            i, s = v - 1, v * PIXELS
            centre = s_taps[:, i, 1, g : g + 1]
            if whole:
                affine(u[:, BANK:COLS], late[:], centre, c_inner[:, i, g : g + 1])
                return
            affine(u[:, BANK : COLS - s], late[:, 0 : BANK - s], centre, c_inner[:, i, g : g + 1])
            affine(u[:, COLS - s : COLS], late[:, BANK - s : BANK], centre, c_last[:, i, g : g + 1])

        def outside(dst, v, tap, g):
            nc.gpsimd.tensor_scalar(
                out=dst, in0=dst, scalar1=1.0, scalar2=minus_tap_bias[:, v - 1, tap, g : g + 1], op0=ALU.mult, op1=ALU.add
            )

        def half_pairs(bank):
            return bank[:].rearrange("p (t two q) -> p t two q", two=2, q=PIXELS)

        def light_branch(n, v, g):
            mul, add, sgn = scale[:, v, g : g + 1], offset[:, v, g : g + 1], sign[:, v, g : g + 1]
            m = light_pool.tile([P, OUT_COLS], F32, tag="m")
            m_rows = m[:].rearrange("p (t q) -> p t q", q=PIXELS)
            quarter = TIME // 4
            half_rows = [m_rows[:, 0:quarter, :], m_rows[:, quarter : 2 * quarter, :]]
            pairs = []

            def products(half):
                bank = multiply(n, v, g, half)
                pairs.append(half_pairs(bank))
                if v == 0:
                    scaled_copy(half_rows[half], pairs[half][:, :, 1, :], mul)
                elif half == 0:
                    scaled_copy(m_rows[:, 0 : quarter - 1, :], pairs[0][:, 1:, 0, :], sgn)
                else:
                    scaled_copy(m_rows[:, quarter - 1 : 2 * quarter - 1, :], pairs[1][:, :, 0, :], sgn)
                    scaled_copy(m[:, OUT_COLS - PIXELS : OUT_COLS], bank[:, BANK - PIXELS : BANK], sgn)

            def affine_of(factor):
                return lambda dst: nc.gpsimd.tensor_scalar(
                    out=dst, in0=m[:], scalar1=factor, scalar2=add, op0=ALU.mult, op1=ALU.add
                )

            if v == 0:
                return products, m, [
                    lambda: sttmax(half_rows[0], pairs[0][:, :, 0, :], mul, half_rows[0]),
                    lambda: sttmax(half_rows[1], pairs[1][:, :, 0, :], mul, half_rows[1]),
                ], affine_of(1.0)
            return products, m, [
                lambda: sttmax(half_rows[0], pairs[0][:, :, 0, :], sgn, half_rows[0]),
                lambda: sttmax(half_rows[1], pairs[1][:, :, 0, :], sgn, half_rows[1]),
                lambda: sttmax(half_rows[0], half_rows[0], sgn, pairs[0][:, :, 1, :]),
                lambda: sttmax(half_rows[1], half_rows[1], sgn, pairs[1][:, :, 1, :]),
            ], affine_of(mul)

        def convolution(n, v, g, u=None, early=None, last=False):
            before, after, s = outer_taps(v, g)
            begun = u is not None
            if not begun:
                u = work.tile([P, COLS], F32, tag="u")
            banks = [early]

            def products(half):
                if half == 0:
                    if not begun:
                        banks[0] = multiply(n, v, g, 0)
                        centre_early(u, banks[0], v, g, not last)
                else:
                    banks.append(multiply(n, v, g, 1))
                    centre_late(u, banks[1], v, g, not begun and not last)

            if begun:
                return products, u, [
                    lambda: add_tap(u[:, BANK : BANK + s], banks[0][:, BANK - s : BANK], before),
                    lambda: add_tap(u[:, BANK + s : COLS], banks[1][:, 0 : BANK - s], before),
                    lambda: add_tap(u[:, BANK - s : BANK], banks[1][:, 0:s], after),
                    lambda: add_tap(u[:, BANK : COLS - s], banks[1][:, s:BANK], after),
                ], None
            ends = [] if last else [lambda: outside(u[:, COLS - s : COLS], v, 2, g), lambda: outside(u[:, 0:s], v, 0, g)]
            return products, u, [
                lambda: add_tap(u[:, s : s + BANK], banks[0][:], before),
                lambda: add_tap(u[:, s + BANK : COLS], banks[1][:, 0 : BANK - s], before),
                lambda: add_tap(u[:, 0 : BANK - s], banks[0][:, s:BANK], after),
                lambda: add_tap(u[:, BANK - s : COLS - s], banks[1][:], after),
            ] + ends, None

        def pool(u, pieces):
            pooled = pooled_pool.tile([P, OUT_COLS], F32, tag="pooled")
            pairs = u[:].rearrange("p (t two q) -> p t two q", two=2, q=PIXELS)
            steps = TIME // 2 // pieces
            for piece in range(pieces):
                t = slice(piece * steps, (piece + 1) * steps)
                nc.vector.tensor_tensor(
                    out=pooled[:].rearrange("p (t q) -> p t q", q=PIXELS)[:, t, :],
                    in0=pairs[:, t, 0, :],
                    in1=pairs[:, t, 1, :],
                    op=ALU.max,
                )
            return pooled

        def emit(pooled_by_group, n, v, pair):
            flipped = flip_psum.tile([P, 2, GROUPS, P], F32, tag="flip")
            for a in range(2):
                first = (2 * pair + a) * P
                for g in range(GROUPS):
                    nc.tensor.transpose(flipped[:, a, g, :], pooled_by_group[g][:, first : first + P], ident[:])
            out_tile = out_pool.tile([P, 2, GROUPS * CB], F32, tag="out")
            nc.scalar.activation(
                out=out_tile[:].rearrange("p a (o g) -> p a o g", g=GROUPS),
                in_=flipped[:].rearrange("p a g o -> p a o g"),
                func=ACT.Relu,
            )
            rows = out_rows[n * OUT_COLS + pair * CHUNK : n * OUT_COLS + (pair + 1) * CHUNK, :]
            channels = rows[:, v * GROUPS * CB : (v + 1) * GROUPS * CB]
            nc.sync.dma_start(out=channels.rearrange("(a p) c -> p a c", p=P), in_=out_tile[:])

        def turn_piece(flipped, g, pooled, piece):
            nc.tensor.transpose(flipped[:, g, :], pooled[:, piece * P : (piece + 1) * P], ident[:])

        def store_piece(flipped, n, v, piece):
            out_tile = out_pool.tile([P, GROUPS * CB], F32, tag="piece")
            shuffled = out_tile[:].rearrange("p (o g) -> p o g", g=GROUPS)
            if piece % 2 == 0:
                nc.scalar.activation(out=shuffled, in_=flipped[:].rearrange("p g o -> p o g"), func=ACT.Relu)
            else:
                nc.vector.tensor_scalar_max(out=shuffled, in0=flipped[:].rearrange("p g o -> p o g"), scalar1=0.0)
            first = n * OUT_COLS + piece * P
            nc.sync.dma_start(out=out_rows[first : first + P, v * GROUPS * CB : (v + 1) * GROUPS * CB], in_=out_tile[:])

        units = []
        for n in range(BATCH - 1):
            for g in range(GROUPS):
                units.extend([(n, v, g) for v in (FIRST_ORDER if n + g == 0 else BRANCH_ORDER)])
        units.extend([(BATCH - 1, v, g) for v, g in LAST_UNITS])

        for chunk in range(CHUNKS):
            load(CHUNKS + chunk)
        load_codes(range(BRANCHES), 1)

        begun = []
        late_quantise = []
        early_taps = []
        for turn, v in enumerate(CONVOLUTIONS):
            bank = multiply(0, v, 0, 0)
            u = work.tile([P, COLS], F32, tag="u")
            centre_early(u, bank, v, 0)
            begun.append((u, bank))
            for index in ((4, 5), (6, 7), ())[turn]:
                late_quantise.append(head_flip(index))
            before, after, s = outer_taps(v, 0)
            early_taps.append(lambda u=u, bank=bank, s=s, tap=before: add_tap(u[:, s:BANK], bank[:, 0 : BANK - s], tap))
            early_taps.append(lambda u=u, bank=bank, s=s, tap=after: add_tap(u[:, 0 : BANK - s], bank[:, s:BANK], tap))
        for turn, tap in enumerate(early_taps):
            tap()
            if turn < len(late_quantise):
                late_quantise[turn]()

        flips = [(part, kp, chunk) for part in range(1, SLICES) for kp in range(PASSES) for chunk in range(CHUNKS)]
        flipped_so_far = 0
        wide = None
        filled = []
        to_quantise = []
        quantised = 0
        first_use = {}
        for place, (n, v, g) in enumerate(units):
            first_use.setdefault(n * GROUPS + g, place)
        to_pool = None
        pooled_tiles = {}
        pooled_now = []
        to_emit = []
        emitted = 0

        def note_pooled(pooled, n, v, g):
            pooled_tiles.setdefault((n, v), {})[g] = pooled
            if len(pooled_tiles[(n, v)]) == GROUPS:
                pooled_now.append((n, v))

        def pool_last(pieces=1):
            u, n, v, g = to_pool
            note_pooled(pool(u, pieces), n, v, g)

        started = []
        for place, (n, v, g) in enumerate(units):
            products = []
            while len(started) < min(place + 1 + LEAD, len(units)):
                unit = units[len(started)]
                if len(started) < len(begun):
                    started.append(convolution(*unit, *begun[len(started)]))
                else:
                    if unit[1] in (0, 4):
                        started.append(light_branch(*unit))
                    else:
                        started.append(convolution(*unit, last=len(started) == len(units) - 1))
                products.extend([(started[-1][0], 0), (started[-1][0], 1)])
            u, steps, finish = started[place][1:]
            waiting = len([item for item in to_emit[emitted:] if item[0] <= place])
            emits = min(waiting, 1 if flipped_so_far < len(flips) else 2)
            turns = TURNS[v] - emits
            banks = [("flip", item) for item in flips[flipped_so_far : flipped_so_far + turns]]
            flipped_so_far += turns
            banks.extend([("emit", item[1]) for item in to_emit[emitted : emitted + emits]])
            emitted += emits
            for product, half in products:
                product(half)
            for kind, item in banks:
                if kind == "emit":
                    emit(*item)
                else:
                    part, kp, chunk = item
                    if kp == 0:
                        load((part + 1) * CHUNKS + chunk)
                    if chunk == 0:
                        wide = wide_pool.tile([P, 4 * COLS], BF16, align_bytes=64, tag="wide")
                    flip(part, kp, chunk, wide[:, 4 * CHUNK * chunk : 4 * CHUNK * (chunk + 1)], "scalar")
                    if chunk == CHUNKS - 1:
                        filled.append((part, kp, slice(0, COLS), wide[:]))
            first_steps = len(steps) if finish is None and place < len(units) - 1 else len(steps) // 2
            for step in steps[:first_steps]:
                step()
            if to_pool is not None:
                pool_last()
            room = {0: 1, 4: 1}.get(v, 0)
            while quantised < len(to_quantise) and (
                room > 0 or first_use[to_quantise[quantised][0]] - QUANTISE_AHEAD <= place
            ):
                quantise(*to_quantise[quantised])
                quantised += 1
                room -= 1
            for step in steps[first_steps:]:
                step()
            to_pool = (u, n, v, g)
            if finish is not None:
                pooled = pooled_pool.tile([P, OUT_COLS], F32, tag="pooled")
                finish(pooled[:])
                note_pooled(pooled, n, v, g)
                to_pool = None
            to_quantise.extend(filled)
            filled.clear()
            for key in pooled_now:
                to_emit.extend([(place + 1 + EMIT_LAG, (pooled_tiles[key], key[0], key[1], pair)) for pair in range(2)])
            pooled_now.clear()
        for item in to_emit[emitted:]:
            emit(*item[1])
        u, n, v, g = to_pool
        pieces = []
        for piece in range(OUT_COLS // P):
            flipped = acc_psum.tile([P, GROUPS, P], F32, tag="acc")
            turn_piece(flipped, 1 - g, pooled_tiles[(n, v)][1 - g], piece)
            pieces.append(flipped)
        pooled = pool(u, len(pieces))
        for piece, flipped in enumerate(pieces):
            turn_piece(flipped, g, pooled, piece)
            store_piece(flipped, n, v, piece)
